import numpy as np
import ml_dtypes


def mxq(x, axis, fmt="e4m3"):
    dtype, down = {"e4m3": (ml_dtypes.float8_e4m3fn, 7), "e5m2": (ml_dtypes.float8_e5m2, 14)}[fmt]
    v = np.moveaxis(np.asarray(x, np.float32).astype(ml_dtypes.bfloat16).astype(np.float64), axis, -1)
    blocks = v.reshape(v.shape[:-1] + (-1, 32))
    amax = np.abs(blocks).max(-1, keepdims=True)
    byte = np.maximum(np.where(amax > 0, np.frexp(amax)[1] - 1 + 127, 0) - down, 1)
    scale = np.exp2(byte - 127.0)
    codes = (blocks / scale).astype(np.float32).astype(dtype).astype(np.float64)
    return np.moveaxis((codes * scale).reshape(v.shape), -1, axis)


WIDE = False


def mx_kscale(k):
    if not WIDE:
        return np.ones(k)
    levels = np.array([18, -18])
    if k % 512:
        return np.exp2(np.random.permutation(np.resize(levels, k // 32))).repeat(32)
    a = np.empty((k // 512, 16))
    for p in range(k // 512):
        a[p, :8] = np.random.permutation(np.resize(levels, 8))
        for g in range(8):
            far = levels[np.abs(levels - a[p, g]) >= 10]
            a[p, g + 8] = far[np.random.randint(len(far))]
    return np.exp2(a.ravel()).repeat(32)


BF16 = ml_dtypes.bfloat16


def bf(x):
    return np.asarray(x, np.float32).astype(BF16)


def f64(x):
    return np.asarray(x).astype(np.float64)


B, S, M, D, H = 8, 128, 8, 256, 1024
T = B * S


def aggregate(src, neigh):
    valid = np.any(neigh != 0, axis=-1).astype(np.float64)
    num = np.sum(valid, axis=-1)
    neigh_mean = neigh.sum(axis=2) / np.maximum(num, 1.0)[..., None]
    hidden = np.concatenate([src.sum(axis=2), neigh_mean], axis=-1)
    return hidden.reshape(-1, hidden.shape[-1])


def setup_inputs():
    s = mx_kscale(T)
    u = mx_kscale(H)
    lens = np.random.randint(0, M + 1, (B, S))
    valid = (np.arange(M)[None, None, :] < lens[:, :, None]).astype(np.float64)
    src0 = bf(np.random.standard_normal((B, S, M, D)) / np.sqrt(M))
    neigh0 = bf(np.random.standard_normal((B, S, M, D)) * 2.0 * valid[..., None])
    w0 = bf(np.random.standard_normal((2 * D, H)) / np.sqrt(2 * D))
    b = bf(-0.5 + 0.3 * np.random.standard_normal(H))
    while True:
        z = aggregate(f64(src0), f64(neigh0)) @ f64(w0) + f64(b)
        bad = np.nonzero(np.min(np.abs(z), axis=1) < 1e-5)[0]
        if bad.size == 0:
            break
        src0[bad // S, bad % S] = bf(np.random.standard_normal((bad.size, M, D)) / np.sqrt(M))
    g = bf(4.0 * np.random.standard_normal((T, H)) * np.exp2(np.random.randint(-6, 1, (T, 1))) / s[:, None] * u)
    st = s.reshape(B, S, 1, 1)
    return {"src_node_features": bf(f64(src0) * st), "neigh_node_features": bf(f64(neigh0) * st),
            "W_map": bf(f64(w0) / u), "b_map": b, "z": np.asarray(z, np.float32), "grad_out": g}


def reference(src_node_features, neigh_node_features, W_map, b_map, z, grad_out):
    hidden = aggregate(f64(src_node_features), f64(neigh_node_features))
    dz = f64(grad_out) * np.where(f64(z) >= 0, 1.0, 0.01)
    da = mxq(dz, 1, "e5m2") @ mxq(f64(W_map)[:D], 1, "e4m3").T
    dsrc = np.broadcast_to(da.reshape(B, S, 1, D), (B, S, M, D)).copy()
    dw = mxq(hidden, 0, "e4m3").T @ mxq(dz, 0, "e5m2")
    return dsrc, dw

@@ -1,0 +1,231 @@
+from contextlib import ExitStack
+
+import concourse.mybir as mybir
+from concourse.masks import make_identity
+
+T, SLOTS, D, H = 1024, 8, 256, 1024
+FLOPS = 2 * T * H * D + 2 * T * 2 * D * H
+BYTES = 2 * (T * SLOTS * D * 2) + D * H * 2 + T * H * 4 + T * H * 2 + T * SLOTS * D * 4 + 2 * D * H * 4
+
+F32 = mybir.dt.float32
+BF16 = mybir.dt.bfloat16
+I32 = mybir.dt.int32
+U32 = mybir.dt.uint32
+U8 = mybir.dt.uint8
+E4M3 = mybir.dt.float8_e4m3fn_x4
+E5M2 = mybir.dt.float8_e5m2_x4
+ALU = mybir.AluOpType
+AXIS_X = mybir.AxisListType.X
+
+P = 128
+PACK = 4
+K_PASS = P * PACK
+PASSES = T // K_PASS
+BANK = 512
+NODES_PER_BLOCK = P // SLOTS
+BLOCKS = 16
+CHUNK = BLOCKS * NODES_PER_BLOCK
+SLOPE = 0.01
+MAGNITUDE_BITS = 0x7FFF7FFF
+MEAN_SCALE = 29 / 32
+
+
+def tile_syntacticgcn_v_kernel(tc, src, neigh, W_map, b_map, z, grad_out, out_0, out_1):
+    nc = tc.nc
+    with ExitStack() as ctx:
+        keep = ctx.enter_context(tc.tile_pool(name="keep", bufs=1))
+        work = ctx.enter_context(tc.tile_pool(name="work", bufs=2))
+        psum = ctx.enter_context(tc.psum_pool(name="psum", bufs=2))
+        ctx.enter_context(tc.manual_schedule(engines={mybir.EngineType.SP}))
+
+        w_raw = keep.tile([P, 2 * H], BF16, name="w_raw")
+        nc.sync.dma_start(out=w_raw[:], in_=W_map[0:D, :].rearrange("(p e) h -> p (e h)", e=2))
+        z_rows = z.rearrange("(g p j) h -> g p (j h)", p=P, j=PACK)
+        g_rows = grad_out.rearrange("(g p j) h -> g p (j h)", p=P, j=PACK)
+        z_sb = {}
+        dz = []
+        for g in range(PASSES):
+            for half in range(2):
+                z_half = keep.tile([P, 2 * H], F32, name="z%d%d" % (g, half))
+                nc.sync.dma_start(out=z_half[:], in_=z_rows[g, :, half * 2 * H : (half + 1) * 2 * H])
+                z_sb[g, half] = z_half
+                if half == 0:
+                    g_pass = keep.tile([P, PACK * H], BF16, name="dz%d" % g)
+                    nc.sync.dma_start(out=g_pass[:], in_=g_rows[g])
+                    dz.append(g_pass)
+        feats = {}
+        for name, tensor in (("neigh", neigh), ("src", src)):
+            rows = tensor.rearrange("b s m d -> (b s m) d").rearrange("(q k r) d -> q r k d", k=BLOCKS, r=P)
+            for q in range(T // CHUNK):
+                chunk = keep.tile([P, BLOCKS, D], BF16, name="%s%d" % (name, q))
+                nc.sync.dma_start(out=chunk[:], in_=rows[q])
+                feats[name, q] = chunk
+
+        ident = keep.tile([P, P], F32, name="ident")
+        make_identity(nc, ident[:])
+        node_of_row_f = keep.tile([P, NODES_PER_BLOCK], F32, name="node_of_row_f")
+        nc.vector.tensor_reduce(out=node_of_row_f[:], in_=ident[:].rearrange("p (i s) -> p i s", s=SLOTS), axis=AXIS_X, op=ALU.add)
+        node_of_row = keep.tile([P, NODES_PER_BLOCK], BF16, name="node_of_row")
+        nc.vector.tensor_copy(out=node_of_row[:], in_=node_of_row_f[:])
+        quad_of_row = keep.tile([P, PACK], F32, name="quad_of_row")
+        nc.vector.tensor_reduce(out=quad_of_row[:], in_=node_of_row_f[:].rearrange("p (a j) -> p a j", j=PACK), axis=AXIS_X, op=ALU.add)
+        place_of_row_f = keep.tile([P, PACK], F32, name="place_of_row_f")
+        nc.vector.tensor_reduce(out=place_of_row_f[:], in_=node_of_row_f[:].rearrange("p (a j) -> p j a", j=PACK), axis=AXIS_X, op=ALU.add)
+        place_of_row = keep.tile([P, PACK], BF16, name="place_of_row")
+        nc.vector.tensor_scalar(out=place_of_row[:], in0=place_of_row_f[:], scalar1=MEAN_SCALE, scalar2=None, op0=ALU.mult)
+        node_of_row_scaled = keep.tile([P, NODES_PER_BLOCK], BF16, name="node_of_row_scaled")
+        nc.vector.tensor_scalar(out=node_of_row_scaled[:], in0=node_of_row_f[:], scalar1=MEAN_SCALE, scalar2=None, op0=ALU.mult)
+
+        w_codes = keep.tile([P, 2 * BANK], U32, name="w_codes", align_bytes=64)
+        w_scales = keep.tile([P, 2 * BANK], U8, name="w_scales", align_bytes=64)
+        w_words = w_raw[:].bitcast(F32)
+        for hp in range(2):
+            bank = psum.tile([P, BANK], F32, name="tr", tag="tr")
+            for e in range(2):
+                for u in range(2):
+                    lo = e * 512 + hp * 256 + u
+                    nc.tensor.transpose(bank[:, (2 * e + u) * P : (2 * e + u + 1) * P], w_words[:, lo : e * 512 + (hp + 1) * 256 : 2], ident[:])
+            grouped = work.tile([P, 4 * D], BF16, name="grouped", tag="grouped", align_bytes=64)
+            nc.scalar.copy(
+                out=grouped[:].bitcast(F32).rearrange("k (p e u) -> k p e u", e=2, u=2),
+                in_=bank[:].rearrange("k (e u p) -> k p e u", e=2, u=2),
+            )
+            for rep in range(2):
+                cols = slice(hp * BANK + rep * D, hp * BANK + (rep + 1) * D)
+                nc.vector.quantize_mx(out=w_codes[:, cols].bitcast(E4M3), scales=w_scales[:, cols], in_=grouped[:])
+
+        out0_rows = out_0.rearrange("b s m d -> (b s) (m d)").rearrange("(g p j) (r n) -> g j p r n", p=P, j=PACK, n=BANK)
+        for g in range(PASSES):
+            for j in range(PACK):
+                cols = slice(j * H, (j + 1) * H)
+                factor = work.tile([P, H], F32, name="factor")
+                nc.vector.tensor_scalar(
+                    out=factor[:], in0=z_sb[g, j // 2][:, (j % 2) * H : (j % 2 + 1) * H],
+                    scalar1=0.0, scalar2=SLOPE, op0=ALU.is_ge, op1=ALU.max,
+                )
+                nc.vector.tensor_tensor(out=dz[g][:, cols], in0=dz[g][:, cols], in1=factor[:], op=ALU.mult)
+                words = dz[g][:, cols].bitcast(F32)
+                bank = psum.tile([P, BANK], F32, name="tr", tag="tr")
+                for hp in range(2):
+                    for u in range(2):
+                        nc.tensor.transpose(bank[:, (2 * hp + u) * P : (2 * hp + u + 1) * P], words[:, hp * 256 + u : (hp + 1) * 256 : 2], ident[:])
+                grouped = work.tile([P, 4 * D], BF16, name="grouped", tag="grouped", align_bytes=64)
+                nc.scalar.copy(
+                    out=grouped[:].bitcast(F32).rearrange("k (hp r u) -> k hp r u", hp=2, u=2),
+                    in_=bank[:].rearrange("k (hp u r) -> k hp r u", hp=2, u=2),
+                )
+                dzt_codes = work.tile([P, 2 * P], U32, name="dzt_codes", align_bytes=64)
+                dzt_scales = work.tile([P, 2 * P], U8, name="dzt_scales", align_bytes=64)
+                nc.vector.quantize_mx(out=dzt_codes[:].bitcast(E5M2), scales=dzt_scales[:], in_=grouped[:])
+                acc = psum.tile([P, BANK], F32, name="acc", tag="acc")
+                for hp in range(2):
+                    nc.tensor.matmul_mx(
+                        out=acc[:],
+                        lhsT=dzt_codes[:, hp * P : (hp + 1) * P].bitcast(E5M2),
+                        lhsT_scale=dzt_scales[:, hp * P : (hp + 1) * P],
+                        rhs=w_codes[:, hp * BANK : (hp + 1) * BANK].bitcast(E4M3),
+                        rhs_scale=w_scales[:, hp * BANK : (hp + 1) * BANK],
+                        start=(hp == 0), stop=(hp == 1),
+                    )
+                da_twice = keep.tile([P, BANK], F32, name="da%d%d" % (g, j))
+                nc.scalar.copy(out=da_twice[:], in_=acc[:])
+                nc.sync.dma_start(out=out0_rows[g, j], in_=da_twice[:].unsqueeze(1).broadcast_to([P, SLOTS // 2, BANK]))
+
+        def slot_sums(chunk, selector):
+            bank = psum.tile([P, BANK], F32, name="sums", tag="sums", bufs=3)
+            for cc in range(2):
+                for k in range(BLOCKS):
+                    at = cc * CHUNK + k * NODES_PER_BLOCK
+                    nc.tensor.matmul(bank[:, at : at + NODES_PER_BLOCK], lhsT=chunk[:, k, cc * P : (cc + 1) * P], rhs=selector[:], start=True, stop=True)
+            return bank
+
+        h_codes = [keep.tile([P, 2 * D], U32, name="h_codes%d" % g, align_bytes=64) for g in range(PASSES)]
+        h_scales = [keep.tile([P, 2 * D], U8, name="h_scales%d" % g, align_bytes=64) for g in range(PASSES)]
+        dz_codes = [keep.tile([P, H], U32, name="dz_codes%d" % g, align_bytes=64) for g in range(PASSES)]
+        dz_scales = [keep.tile([P, H], U8, name="dz_scales%d" % g, align_bytes=64) for g in range(PASSES)]
+
+        for g in range(PASSES):
+            sums_t = work.tile([P, 2, PACK, P], F32, name="sums_t")
+            peak = work.tile([P, 2 * BLOCKS], F32, name="peak")
+            for half in range(2):
+                chunk = feats["neigh", 2 * g + half]
+                bank = slot_sums(chunk, node_of_row_scaled)
+                nc.scalar.copy(
+                    out=sums_t[:, :, :, half * 64 : (half + 1) * 64],
+                    in_=bank[:].rearrange("c (cc p j) -> c cc j p", cc=2, j=PACK),
+                )
+                bits = chunk[:].rearrange("r k d -> r (k d)").bitcast(I32).rearrange("r (k w) -> r k w", k=BLOCKS)
+                folded = work.tile([P, BLOCKS, 64], I32, name="folded")
+                nc.vector.tensor_tensor(out=folded[:], in0=bits[:, :, 0:64], in1=bits[:, :, 64:128], op=ALU.bitwise_or)
+                for width in (32, 16, 8):
+                    nc.vector.tensor_tensor(out=folded[:, :, 0:width], in0=folded[:, :, 0:width], in1=folded[:, :, width : 2 * width], op=ALU.bitwise_or)
+                magnitude = work.tile([P, BLOCKS, 8], I32, name="magnitude")
+                nc.vector.tensor_scalar(out=magnitude[:], in0=folded[:, :, 0:8], scalar1=MAGNITUDE_BITS, scalar2=None, op0=ALU.bitwise_and)
+                nc.vector.tensor_reduce(out=peak[:, half * BLOCKS : (half + 1) * BLOCKS], in_=magnitude[:], axis=AXIS_X, op=ALU.max)
+            spread = work.tile([P, 2 * BLOCKS, PACK], BF16, name="spread")
+            nc.vector.scalar_tensor_tensor(
+                out=spread[:], in0=peak[:].unsqueeze(2).broadcast_to([P, 2 * BLOCKS, PACK]), scalar=0.0,
+                in1=quad_of_row[:].unsqueeze(1).broadcast_to([P, 2 * BLOCKS, PACK]), op0=ALU.is_gt, op1=ALU.mult,
+            )
+            count = psum.tile([P, PACK], F32, name="count", tag="count", bufs=1)
+            nc.tensor.matmul(count[:], lhsT=spread[:].rearrange("r k a -> r (k a)"), rhs=place_of_row[:], start=True, stop=True)
+            divisor = work.tile([P, PACK], F32, name="divisor")
+            nc.vector.tensor_scalar(out=divisor[:], in0=count[:], scalar1=MEAN_SCALE, scalar2=None, op0=ALU.max)
+            inverse = work.tile([P, PACK], F32, name="inverse")
+            nc.vector.reciprocal(out=inverse[:], in_=divisor[:])
+            mean = work.tile([P, D * PACK], BF16, name="mean", tag="grouped", align_bytes=64)
+            for cc in range(2):
+                bank = psum.tile([P, BANK], F32, name="tr", tag="tr")
+                for j in range(PACK):
+                    nc.tensor.transpose(bank[:, j * P : (j + 1) * P], sums_t[:, cc, j, :], ident[:])
+                nc.vector.tensor_tensor(
+                    out=mean[:, cc * K_PASS : (cc + 1) * K_PASS].rearrange("p (c j) -> p c j", j=PACK),
+                    in0=bank[:].rearrange("p (j c) -> p c j", j=PACK),
+                    in1=inverse[:].unsqueeze(1).broadcast_to([P, P, PACK]),
+                    op=ALU.mult,
+                )
+            nc.vector.quantize_mx(out=h_codes[g][:, D : 2 * D].bitcast(E4M3), scales=h_scales[g][:, D : 2 * D], in_=mean[:])
+
+            for n in range(2):
+                woven = work.tile([P, BANK * PACK], BF16, name="woven", align_bytes=64)
+                nc.scalar.copy(
+                    out=woven[:].rearrange("p (c i t) -> p c t i", i=4, t=PACK),
+                    in_=dz[g][:].rearrange("p (t h) -> p t h", t=PACK)[:, :, n * BANK : (n + 1) * BANK].rearrange("p t (c i) -> p c t i", i=4),
+                )
+                cols = slice(n * BANK, (n + 1) * BANK)
+                nc.vector.quantize_mx(out=dz_codes[g][:, cols].bitcast(E5M2), scales=dz_scales[g][:, cols], in_=woven[:])
+
+        for g in range(PASSES):
+            pairs = work.tile([P, 2, 2, P, 2], BF16, name="pairs")
+            for half in range(2):
+                bank = slot_sums(feats["src", 2 * g + half], node_of_row)
+                nc.scalar.copy(
+                    out=pairs[:, :, :, half * 64 : (half + 1) * 64, :],
+                    in_=bank[:].rearrange("c (cc w u e) -> c cc u w e", cc=2, u=2, e=2),
+                )
+            words = pairs[:].rearrange("c cc u w e -> c (cc u w e)").bitcast(F32)
+            bank = psum.tile([P, BANK], F32, name="tr", tag="tr")
+            for i in range(4):
+                nc.tensor.transpose(bank[:, i * P : (i + 1) * P], words[:, i * P : (i + 1) * P], ident[:])
+            total = work.tile([P, D * PACK], BF16, name="total", tag="grouped", align_bytes=64)
+            nc.scalar.copy(
+                out=total[:].bitcast(F32).rearrange("p (cc c u) -> p cc c u", cc=2, u=2),
+                in_=bank[:].rearrange("p (cc u c) -> p cc c u", cc=2, u=2),
+            )
+            nc.vector.quantize_mx(out=h_codes[g][:, 0:D].bitcast(E4M3), scales=h_scales[g][:, 0:D], in_=total[:])
+
+        for m in (2, 3, 0, 1):
+            rows = slice(m * P, (m + 1) * P)
+            dw = keep.tile([P, H], F32, name="dw%d" % m)
+            for n in range(2):
+                cols = slice(n * BANK, (n + 1) * BANK)
+                acc = psum.tile([P, BANK], F32, name="acc", tag="acc")
+                for g in range(PASSES):
+                    nc.tensor.matmul_mx(
+                        out=acc[:],
+                        lhsT=h_codes[g][:, rows].bitcast(E4M3), lhsT_scale=h_scales[g][:, rows],
+                        rhs=dz_codes[g][:, cols].bitcast(E5M2), rhs_scale=dz_scales[g][:, cols],
+                        start=(g == 0), stop=(g == PASSES - 1),
+                    )
+                nc.scalar.copy(out=dw[:, cols], in_=acc[:])
+            nc.sync.dma_start(out=out_1[rows, :], in_=dw[:])

@@ -22,9 +22,11 @@ PACK = 4
 K_PASS = P * PACK
 PASSES = T // K_PASS
 BANK = 512
-NODES_PER_BLOCK = P // SLOTS
-BLOCKS = 16
+NODES_PER_BLOCK = 2 * P // SLOTS
+BLOCKS = 8
 CHUNK = BLOCKS * NODES_PER_BLOCK
+QUADS = NODES_PER_BLOCK // PACK
+COPIES = 4
 SLOPE = 0.01
 MAGNITUDE_BITS = 0x7FFF7FFF
 MEAN_SCALE = 29 / 32
@@ -38,43 +40,52 @@ def tile_syntacticgcn_v_kernel(tc, src, neigh, W_map, b_map, z, grad_out, out_0,
         psum = ctx.enter_context(tc.psum_pool(name="psum", bufs=2))
         ctx.enter_context(tc.manual_schedule(engines={mybir.EngineType.SP}))
 
-        w_raw = keep.tile([P, 2 * H], BF16, name="w_raw")
-        nc.sync.dma_start(out=w_raw[:], in_=W_map[0:D, :].rearrange("(p e) h -> p (e h)", e=2))
         z_rows = z.rearrange("(g p j) h -> g p (j h)", p=P, j=PACK)
         g_rows = grad_out.rearrange("(g p j) h -> g p (j h)", p=P, j=PACK)
+        w_raw = keep.tile([P, 2 * H], BF16, name="w_raw")
         z_sb = {}
         dz = []
         for g in range(PASSES):
+            g_pass = keep.tile([P, PACK * H], BF16, name="dz%d" % g)
+            dz.append(g_pass)
             for half in range(2):
-                z_half = keep.tile([P, 2 * H], F32, name="z%d%d" % (g, half))
-                nc.sync.dma_start(out=z_half[:], in_=z_rows[g, :, half * 2 * H : (half + 1) * 2 * H])
+                z_half = keep.tile([P, 2 * H], F32, name="z_half", tag="z%d%d" % (g, half))
                 z_sb[g, half] = z_half
-                if half == 0:
-                    g_pass = keep.tile([P, PACK * H], BF16, name="dz%d" % g)
-                    nc.sync.dma_start(out=g_pass[:], in_=g_rows[g])
-                    dz.append(g_pass)
-        feats = {}
-        for name, tensor in (("neigh", neigh), ("src", src)):
-            rows = tensor.rearrange("b s m d -> (b s m) d").rearrange("(q k r) d -> q r k d", k=BLOCKS, r=P)
-            for q in range(T // CHUNK):
-                chunk = keep.tile([P, BLOCKS, D], BF16, name="%s%d" % (name, q))
-                nc.sync.dma_start(out=chunk[:], in_=rows[q])
-                feats[name, q] = chunk
+        nc.sync.dma_start(out=z_sb[0, 0][:, 0:H], in_=z_rows[0, :, 0:H])
+        nc.sync.dma_start(out=dz[0][:, 0 : 2 * H], in_=g_rows[0, :, 0 : 2 * H])
+        nc.sync.dma_start(out=w_raw[:], in_=W_map[0:D, :].rearrange("(p e) h -> p (e h)", e=2))
+        nc.sync.dma_start(out=z_sb[0, 0][:, H : 2 * H], in_=z_rows[0, :, H : 2 * H])
+        nc.sync.dma_start(out=z_sb[0, 1][:], in_=z_rows[0, :, 2 * H :])
+        nc.sync.dma_start(out=dz[0][:, 2 * H :], in_=g_rows[0, :, 2 * H :])
+        nc.sync.dma_start(out=z_sb[1, 0][:], in_=z_rows[1, :, 0 : 2 * H])
+        nc.sync.dma_start(out=dz[1][:], in_=g_rows[1])
+        nc.sync.dma_start(out=z_sb[1, 1][:], in_=z_rows[1, :, 2 * H :])
+        src_rows = src.rearrange("b s m d -> (b s) (m d)").rearrange("(g p u e) x -> g u p (e x)", p=P, u=2, e=2)
+        src_sb = {}
+        for g in range(PASSES):
+            for u in range(2):
+                chunk = keep.tile([P, 2 * SLOTS * D], BF16, name="src%d%d" % (g, u))
+                nc.sync.dma_start(out=chunk[:], in_=src_rows[g, u])
+                src_sb[g, u] = chunk
+        neigh_rows = neigh.rearrange("b s (v e) d -> (b s v) (e d)", e=2).rearrange("(q k r) x -> q r k x", k=BLOCKS, r=P)
+        neigh_sb = []
+        for q in range(T // CHUNK):
+            chunk = keep.tile([P, BLOCKS, 2 * D], BF16, name="neigh%d" % q)
+            nc.sync.dma_start(out=chunk[:], in_=neigh_rows[q])
+            neigh_sb.append(chunk)
 
         ident = keep.tile([P, P], F32, name="ident")
         make_identity(nc, ident[:])
         node_of_row_f = keep.tile([P, NODES_PER_BLOCK], F32, name="node_of_row_f")
-        nc.vector.tensor_reduce(out=node_of_row_f[:], in_=ident[:].rearrange("p (i s) -> p i s", s=SLOTS), axis=AXIS_X, op=ALU.add)
+        nc.vector.tensor_reduce(out=node_of_row_f[:], in_=ident[:].rearrange("p (i v) -> p i v", v=SLOTS // 2), axis=AXIS_X, op=ALU.add)
         node_of_row = keep.tile([P, NODES_PER_BLOCK], BF16, name="node_of_row")
-        nc.vector.tensor_copy(out=node_of_row[:], in_=node_of_row_f[:])
-        quad_of_row = keep.tile([P, PACK], F32, name="quad_of_row")
+        nc.vector.tensor_scalar(out=node_of_row[:], in0=node_of_row_f[:], scalar1=MEAN_SCALE, scalar2=None, op0=ALU.mult)
+        quad_of_row = keep.tile([P, QUADS], F32, name="quad_of_row")
         nc.vector.tensor_reduce(out=quad_of_row[:], in_=node_of_row_f[:].rearrange("p (a j) -> p a j", j=PACK), axis=AXIS_X, op=ALU.add)
         place_of_row_f = keep.tile([P, PACK], F32, name="place_of_row_f")
         nc.vector.tensor_reduce(out=place_of_row_f[:], in_=node_of_row_f[:].rearrange("p (a j) -> p j a", j=PACK), axis=AXIS_X, op=ALU.add)
         place_of_row = keep.tile([P, PACK], BF16, name="place_of_row")
         nc.vector.tensor_scalar(out=place_of_row[:], in0=place_of_row_f[:], scalar1=MEAN_SCALE, scalar2=None, op0=ALU.mult)
-        node_of_row_scaled = keep.tile([P, NODES_PER_BLOCK], BF16, name="node_of_row_scaled")
-        nc.vector.tensor_scalar(out=node_of_row_scaled[:], in0=node_of_row_f[:], scalar1=MEAN_SCALE, scalar2=None, op0=ALU.mult)
 
         w_codes = keep.tile([P, 2 * BANK], U32, name="w_codes", align_bytes=64)
         w_scales = keep.tile([P, 2 * BANK], U8, name="w_scales", align_bytes=64)
@@ -94,16 +105,13 @@ def tile_syntacticgcn_v_kernel(tc, src, neigh, W_map, b_map, z, grad_out, out_0,
                 cols = slice(hp * BANK + rep * D, hp * BANK + (rep + 1) * D)
                 nc.vector.quantize_mx(out=w_codes[:, cols].bitcast(E4M3), scales=w_scales[:, cols], in_=grouped[:])
 
-        out0_rows = out_0.rearrange("b s m d -> (b s) (m d)").rearrange("(g p j) (r n) -> g j p r n", p=P, j=PACK, n=BANK)
+        out0_rows = out_0.rearrange("b s m d -> (b s) (m d)").rearrange("(g p j) (r n) -> g j p r n", p=P, j=PACK, n=COPIES * D)
         for g in range(PASSES):
             for j in range(PACK):
                 cols = slice(j * H, (j + 1) * H)
-                factor = work.tile([P, H], F32, name="factor")
-                nc.vector.tensor_scalar(
-                    out=factor[:], in0=z_sb[g, j // 2][:, (j % 2) * H : (j % 2 + 1) * H],
-                    scalar1=0.0, scalar2=SLOPE, op0=ALU.is_ge, op1=ALU.max,
-                )
-                nc.vector.tensor_tensor(out=dz[g][:, cols], in0=dz[g][:, cols], in1=factor[:], op=ALU.mult)
+                factor = z_sb[g, j // 2][:, (j % 2) * H : (j % 2 + 1) * H]
+                nc.vector.tensor_scalar(out=factor, in0=factor, scalar1=0.0, scalar2=SLOPE, op0=ALU.is_ge, op1=ALU.max)
+                nc.vector.tensor_tensor(out=dz[g][:, cols], in0=dz[g][:, cols], in1=factor, op=ALU.mult)
                 words = dz[g][:, cols].bitcast(F32)
                 bank = psum.tile([P, BANK], F32, name="tr", tag="tr")
                 for hp in range(2):
@@ -127,17 +135,12 @@ def tile_syntacticgcn_v_kernel(tc, src, neigh, W_map, b_map, z, grad_out, out_0,
                         rhs_scale=w_scales[:, hp * BANK : (hp + 1) * BANK],
                         start=(hp == 0), stop=(hp == 1),
                     )
-                da_twice = keep.tile([P, BANK], F32, name="da%d%d" % (g, j))
-                nc.scalar.copy(out=da_twice[:], in_=acc[:])
-                nc.sync.dma_start(out=out0_rows[g, j], in_=da_twice[:].unsqueeze(1).broadcast_to([P, SLOTS // 2, BANK]))
-
-        def slot_sums(chunk, selector):
-            bank = psum.tile([P, BANK], F32, name="sums", tag="sums", bufs=3)
-            for cc in range(2):
-                for k in range(BLOCKS):
-                    at = cc * CHUNK + k * NODES_PER_BLOCK
-                    nc.tensor.matmul(bank[:, at : at + NODES_PER_BLOCK], lhsT=chunk[:, k, cc * P : (cc + 1) * P], rhs=selector[:], start=True, stop=True)
-            return bank
+                da_copies = keep.tile([P, COPIES * D], F32, name="da%d%d" % (g, j))
+                nc.scalar.copy(
+                    out=da_copies[:].rearrange("p (r n) -> p r n", n=BANK),
+                    in_=acc[:].unsqueeze(1).broadcast_to([P, COPIES // 2, BANK]),
+                )
+                nc.sync.dma_start(out=out0_rows[g, j], in_=da_copies[:].unsqueeze(1).broadcast_to([P, SLOTS // COPIES, COPIES * D]))
 
         h_codes = [keep.tile([P, 2 * D], U32, name="h_codes%d" % g, align_bytes=64) for g in range(PASSES)]
         h_scales = [keep.tile([P, 2 * D], U8, name="h_scales%d" % g, align_bytes=64) for g in range(PASSES)]
@@ -145,30 +148,78 @@ def tile_syntacticgcn_v_kernel(tc, src, neigh, W_map, b_map, z, grad_out, out_0,
         dz_scales = [keep.tile([P, H], U8, name="dz_scales%d" % g, align_bytes=64) for g in range(PASSES)]
 
         for g in range(PASSES):
+            pairs = work.tile([P, 2, 2, P, 2], BF16, name="pairs")
+            for u in range(2):
+                bank = psum.tile([P, BANK], F32, name="sums", tag="sums", bufs=3)
+                for e in range(2):
+                    node = src_sb[g, u][:, e * SLOTS * D : (e + 1) * SLOTS * D]
+                    partial = work.tile([P, SLOTS // 2 * D], F32, name="partial", bufs=3)
+                    nc.vector.tensor_tensor(out=partial[:], in0=node[:, 0 : SLOTS // 2 * D], in1=node[:, SLOTS // 2 * D :], op=ALU.add)
+                    for cc in range(2):
+                        at = (2 * cc + e) * P
+                        for v in range(SLOTS // 2):
+                            nc.tensor.matmul(
+                                bank[:, at : at + P], lhsT=partial[:, v * D + cc * P : v * D + (cc + 1) * P], rhs=ident[:],
+                                is_transpose=True, start=(v == 0), stop=(v == SLOTS // 2 - 1),
+                            )
+                nc.scalar.copy(out=pairs[:, :, u, :, :], in_=bank[:].rearrange("c (cc e w) -> c cc w e", cc=2, e=2))
+            words = pairs[:].rearrange("c cc u w e -> c (cc u w e)").bitcast(F32)
+            bank = psum.tile([P, BANK], F32, name="tr", tag="tr")
+            for i in range(4):
+                nc.tensor.transpose(bank[:, i * P : (i + 1) * P], words[:, i * P : (i + 1) * P], ident[:])
+            total = work.tile([P, D * PACK], BF16, name="total", tag="grouped", align_bytes=64)
+            nc.scalar.copy(
+                out=total[:].bitcast(F32).rearrange("p (cc c u) -> p cc c u", cc=2, u=2),
+                in_=bank[:].rearrange("p (cc u c) -> p cc c u", cc=2, u=2),
+            )
+            nc.vector.quantize_mx(out=h_codes[g][:, 0:D].bitcast(E4M3), scales=h_scales[g][:, 0:D], in_=total[:])
+
+            for n in range(2):
+                woven = work.tile([P, BANK * PACK], BF16, name="woven", align_bytes=64)
+                nc.scalar.copy(
+                    out=woven[:].rearrange("p (c i t) -> p c t i", i=4, t=PACK),
+                    in_=dz[g][:].rearrange("p (t h) -> p t h", t=PACK)[:, :, n * BANK : (n + 1) * BANK].rearrange("p t (c i) -> p c t i", i=4),
+                )
+                cols = slice(n * BANK, (n + 1) * BANK)
+                nc.vector.quantize_mx(out=dz_codes[g][:, cols].bitcast(E5M2), scales=dz_scales[g][:, cols], in_=woven[:])
+
+        for g in range(PASSES):
             sums_t = work.tile([P, 2, PACK, P], F32, name="sums_t")
-            peak = work.tile([P, 2 * BLOCKS], F32, name="peak")
+            peak = work.tile([P, 2 * BLOCKS, 2], F32, name="peak")
             for half in range(2):
-                chunk = feats["neigh", 2 * g + half]
-                bank = slot_sums(chunk, node_of_row_scaled)
+                chunk = neigh_sb[2 * g + half]
+                bank = psum.tile([P, BANK], F32, name="sums", tag="sums", bufs=3)
+                for cc in range(2):
+                    for k in range(BLOCKS):
+                        at = cc * CHUNK + k * NODES_PER_BLOCK
+                        for e in range(2):
+                            nc.tensor.matmul(
+                                bank[:, at : at + NODES_PER_BLOCK], lhsT=chunk[:, k, e * D + cc * P : e * D + (cc + 1) * P],
+                                rhs=node_of_row[:], start=(e == 0), stop=(e == 1),
+                            )
                 nc.scalar.copy(
                     out=sums_t[:, :, :, half * 64 : (half + 1) * 64],
                     in_=bank[:].rearrange("c (cc p j) -> c cc j p", cc=2, j=PACK),
                 )
-                bits = chunk[:].rearrange("r k d -> r (k d)").bitcast(I32).rearrange("r (k w) -> r k w", k=BLOCKS)
-                folded = work.tile([P, BLOCKS, 64], I32, name="folded")
+                bits = chunk[:].rearrange("r k x -> r (k x)").bitcast(I32).rearrange("r (k w) -> r k w", k=2 * BLOCKS)
+                folded = work.tile([P, 2 * BLOCKS, 64], I32, name="folded")
                 nc.vector.tensor_tensor(out=folded[:], in0=bits[:, :, 0:64], in1=bits[:, :, 64:128], op=ALU.bitwise_or)
                 for width in (32, 16, 8):
                     nc.vector.tensor_tensor(out=folded[:, :, 0:width], in0=folded[:, :, 0:width], in1=folded[:, :, width : 2 * width], op=ALU.bitwise_or)
-                magnitude = work.tile([P, BLOCKS, 8], I32, name="magnitude")
+                magnitude = work.tile([P, 2 * BLOCKS, 8], I32, name="magnitude")
                 nc.vector.tensor_scalar(out=magnitude[:], in0=folded[:, :, 0:8], scalar1=MAGNITUDE_BITS, scalar2=None, op0=ALU.bitwise_and)
-                nc.vector.tensor_reduce(out=peak[:, half * BLOCKS : (half + 1) * BLOCKS], in_=magnitude[:], axis=AXIS_X, op=ALU.max)
-            spread = work.tile([P, 2 * BLOCKS, PACK], BF16, name="spread")
-            nc.vector.scalar_tensor_tensor(
-                out=spread[:], in0=peak[:].unsqueeze(2).broadcast_to([P, 2 * BLOCKS, PACK]), scalar=0.0,
-                in1=quad_of_row[:].unsqueeze(1).broadcast_to([P, 2 * BLOCKS, PACK]), op0=ALU.is_gt, op1=ALU.mult,
-            )
+                nc.vector.tensor_reduce(
+                    out=peak[:, half * BLOCKS : (half + 1) * BLOCKS, :].rearrange("r k e -> r (k e)"), in_=magnitude[:], axis=AXIS_X, op=ALU.max,
+                )
+            spread = work.tile([P, 2, 2 * BLOCKS, QUADS], BF16, name="spread")
+            for e in range(2):
+                nc.vector.scalar_tensor_tensor(
+                    out=spread[:, e], in0=peak[:, :, e : e + 1].broadcast_to([P, 2 * BLOCKS, QUADS]), scalar=0.0,
+                    in1=quad_of_row[:].unsqueeze(1).broadcast_to([P, 2 * BLOCKS, QUADS]), op0=ALU.is_gt, op1=ALU.mult,
+                )
             count = psum.tile([P, PACK], F32, name="count", tag="count", bufs=1)
-            nc.tensor.matmul(count[:], lhsT=spread[:].rearrange("r k a -> r (k a)"), rhs=place_of_row[:], start=True, stop=True)
+            for e in range(2):
+                nc.tensor.matmul(count[:], lhsT=spread[:, e].rearrange("r k a -> r (k a)"), rhs=place_of_row[:], start=(e == 0), stop=(e == 1))
             divisor = work.tile([P, PACK], F32, name="divisor")
             nc.vector.tensor_scalar(out=divisor[:], in0=count[:], scalar1=MEAN_SCALE, scalar2=None, op0=ALU.max)
             inverse = work.tile([P, PACK], F32, name="inverse")
@@ -186,37 +237,9 @@ def tile_syntacticgcn_v_kernel(tc, src, neigh, W_map, b_map, z, grad_out, out_0,
                 )
             nc.vector.quantize_mx(out=h_codes[g][:, D : 2 * D].bitcast(E4M3), scales=h_scales[g][:, D : 2 * D], in_=mean[:])
 
-            for n in range(2):
-                woven = work.tile([P, BANK * PACK], BF16, name="woven", align_bytes=64)
-                nc.scalar.copy(
-                    out=woven[:].rearrange("p (c i t) -> p c t i", i=4, t=PACK),
-                    in_=dz[g][:].rearrange("p (t h) -> p t h", t=PACK)[:, :, n * BANK : (n + 1) * BANK].rearrange("p t (c i) -> p c t i", i=4),
-                )
-                cols = slice(n * BANK, (n + 1) * BANK)
-                nc.vector.quantize_mx(out=dz_codes[g][:, cols].bitcast(E5M2), scales=dz_scales[g][:, cols], in_=woven[:])
-
-        for g in range(PASSES):
-            pairs = work.tile([P, 2, 2, P, 2], BF16, name="pairs")
-            for half in range(2):
-                bank = slot_sums(feats["src", 2 * g + half], node_of_row)
-                nc.scalar.copy(
-                    out=pairs[:, :, :, half * 64 : (half + 1) * 64, :],
-                    in_=bank[:].rearrange("c (cc w u e) -> c cc u w e", cc=2, u=2, e=2),
-                )
-            words = pairs[:].rearrange("c cc u w e -> c (cc u w e)").bitcast(F32)
-            bank = psum.tile([P, BANK], F32, name="tr", tag="tr")
-            for i in range(4):
-                nc.tensor.transpose(bank[:, i * P : (i + 1) * P], words[:, i * P : (i + 1) * P], ident[:])
-            total = work.tile([P, D * PACK], BF16, name="total", tag="grouped", align_bytes=64)
-            nc.scalar.copy(
-                out=total[:].bitcast(F32).rearrange("p (cc c u) -> p cc c u", cc=2, u=2),
-                in_=bank[:].rearrange("p (cc u c) -> p cc c u", cc=2, u=2),
-            )
-            nc.vector.quantize_mx(out=h_codes[g][:, 0:D].bitcast(E4M3), scales=h_scales[g][:, 0:D], in_=total[:])
-
-        for m in (2, 3, 0, 1):
+        for i, m in enumerate((0, 1, 2, 3)):
             rows = slice(m * P, (m + 1) * P)
-            dw = keep.tile([P, H], F32, name="dw%d" % m)
+            dw = keep.tile([P, H], F32, name="dw", tag="z%d%d" % (i // 2, i % 2))
             for n in range(2):
                 cols = slice(n * BANK, (n + 1) * BANK)
                 acc = psum.tile([P, BANK], F32, name="acc", tag="acc")

@@ -38,7 +38,7 @@ def tile_syntacticgcn_v_kernel(tc, src, neigh, W_map, b_map, z, grad_out, out_0,
         keep = ctx.enter_context(tc.tile_pool(name="keep", bufs=1))
         work = ctx.enter_context(tc.tile_pool(name="work", bufs=2))
         psum = ctx.enter_context(tc.psum_pool(name="psum", bufs=2))
-        ctx.enter_context(tc.manual_schedule(engines={mybir.EngineType.SP}))
+        ctx.enter_context(tc.manual_schedule())
 
         z_rows = z.rearrange("(g p j) h -> g p (j h)", p=P, j=PACK)
         g_rows = grad_out.rearrange("(g p j) h -> g p (j h)", p=P, j=PACK)
@@ -51,28 +51,26 @@ def tile_syntacticgcn_v_kernel(tc, src, neigh, W_map, b_map, z, grad_out, out_0,
             for half in range(2):
                 z_half = keep.tile([P, 2 * H], F32, name="z_half", tag="z%d%d" % (g, half))
                 z_sb[g, half] = z_half
+        nc.sync.dma_start(out=w_raw[:], in_=W_map[0:D, :].rearrange("(p e) h -> p (e h)", e=2))
         nc.sync.dma_start(out=z_sb[0, 0][:, 0:H], in_=z_rows[0, :, 0:H])
         nc.sync.dma_start(out=dz[0][:, 0 : 2 * H], in_=g_rows[0, :, 0 : 2 * H])
-        nc.sync.dma_start(out=w_raw[:], in_=W_map[0:D, :].rearrange("(p e) h -> p (e h)", e=2))
         nc.sync.dma_start(out=z_sb[0, 0][:, H : 2 * H], in_=z_rows[0, :, H : 2 * H])
-        nc.sync.dma_start(out=z_sb[0, 1][:], in_=z_rows[0, :, 2 * H :])
-        nc.sync.dma_start(out=dz[0][:, 2 * H :], in_=g_rows[0, :, 2 * H :])
-        nc.sync.dma_start(out=z_sb[1, 0][:], in_=z_rows[1, :, 0 : 2 * H])
-        nc.sync.dma_start(out=dz[1][:], in_=g_rows[1])
-        nc.sync.dma_start(out=z_sb[1, 1][:], in_=z_rows[1, :, 2 * H :])
+        for g, half in ((0, 1), (1, 0), (1, 1)):
+            cols = slice(half * 2 * H, (half + 1) * 2 * H)
+            nc.sync.dma_start(out=z_sb[g, half][:], in_=z_rows[g, :, cols])
+            nc.sync.dma_start(out=dz[g][:, cols], in_=g_rows[g, :, cols])
         src_rows = src.rearrange("b s m d -> (b s) (m d)").rearrange("(g p u e) x -> g u p (e x)", p=P, u=2, e=2)
-        src_sb = {}
+        neigh_rows = neigh.rearrange("b s (v e) d -> (b s v) (e d)", e=2).rearrange("(q k r) x -> q r k x", k=BLOCKS, r=P)
+        src_sb, neigh_sb = {}, []
         for g in range(PASSES):
             for u in range(2):
-                chunk = keep.tile([P, 2 * SLOTS * D], BF16, name="src%d%d" % (g, u))
-                nc.sync.dma_start(out=chunk[:], in_=src_rows[g, u])
-                src_sb[g, u] = chunk
-        neigh_rows = neigh.rearrange("b s (v e) d -> (b s v) (e d)", e=2).rearrange("(q k r) x -> q r k x", k=BLOCKS, r=P)
-        neigh_sb = []
+                src_chunk = keep.tile([P, 2 * SLOTS * D], BF16, name="src%d%d" % (g, u))
+                nc.sync.dma_start(out=src_chunk[:], in_=src_rows[g, u])
+                src_sb[g, u] = src_chunk
         for q in range(T // CHUNK):
-            chunk = keep.tile([P, BLOCKS, 2 * D], BF16, name="neigh%d" % q)
-            nc.sync.dma_start(out=chunk[:], in_=neigh_rows[q])
-            neigh_sb.append(chunk)
+            neigh_chunk = keep.tile([P, BLOCKS, 2 * D], BF16, name="neigh%d" % q)
+            nc.sync.dma_start(out=neigh_chunk[:], in_=neigh_rows[q])
+            neigh_sb.append(neigh_chunk)
 
         ident = keep.tile([P, P], F32, name="ident")
         make_identity(nc, ident[:])
@@ -89,166 +87,286 @@ def tile_syntacticgcn_v_kernel(tc, src, neigh, W_map, b_map, z, grad_out, out_0,
 
         w_codes = keep.tile([P, 2 * BANK], U32, name="w_codes", align_bytes=64)
         w_scales = keep.tile([P, 2 * BANK], U8, name="w_scales", align_bytes=64)
-        w_words = w_raw[:].bitcast(F32)
-        for hp in range(2):
-            bank = psum.tile([P, BANK], F32, name="tr", tag="tr")
-            for e in range(2):
-                for u in range(2):
-                    lo = e * 512 + hp * 256 + u
-                    nc.tensor.transpose(bank[:, (2 * e + u) * P : (2 * e + u + 1) * P], w_words[:, lo : e * 512 + (hp + 1) * 256 : 2], ident[:])
-            grouped = work.tile([P, 4 * D], BF16, name="grouped", tag="grouped", align_bytes=64)
-            nc.scalar.copy(
-                out=grouped[:].bitcast(F32).rearrange("k (p e u) -> k p e u", e=2, u=2),
-                in_=bank[:].rearrange("k (e u p) -> k p e u", e=2, u=2),
-            )
-            for rep in range(2):
-                cols = slice(hp * BANK + rep * D, hp * BANK + (rep + 1) * D)
-                nc.vector.quantize_mx(out=w_codes[:, cols].bitcast(E4M3), scales=w_scales[:, cols], in_=grouped[:])
-
-        out0_rows = out_0.rearrange("b s m d -> (b s) (m d)").rearrange("(g p j) (r n) -> g j p r n", p=P, j=PACK, n=COPIES * D)
-        for g in range(PASSES):
-            for j in range(PACK):
-                cols = slice(j * H, (j + 1) * H)
-                factor = z_sb[g, j // 2][:, (j % 2) * H : (j % 2 + 1) * H]
-                nc.vector.tensor_scalar(out=factor, in0=factor, scalar1=0.0, scalar2=SLOPE, op0=ALU.is_ge, op1=ALU.max)
-                nc.vector.tensor_tensor(out=dz[g][:, cols], in0=dz[g][:, cols], in1=factor, op=ALU.mult)
-                words = dz[g][:, cols].bitcast(F32)
-                bank = psum.tile([P, BANK], F32, name="tr", tag="tr")
-                for hp in range(2):
-                    for u in range(2):
-                        nc.tensor.transpose(bank[:, (2 * hp + u) * P : (2 * hp + u + 1) * P], words[:, hp * 256 + u : (hp + 1) * 256 : 2], ident[:])
-                grouped = work.tile([P, 4 * D], BF16, name="grouped", tag="grouped", align_bytes=64)
-                nc.scalar.copy(
-                    out=grouped[:].bitcast(F32).rearrange("k (hp r u) -> k hp r u", hp=2, u=2),
-                    in_=bank[:].rearrange("k (hp u r) -> k hp r u", hp=2, u=2),
-                )
-                dzt_codes = work.tile([P, 2 * P], U32, name="dzt_codes", align_bytes=64)
-                dzt_scales = work.tile([P, 2 * P], U8, name="dzt_scales", align_bytes=64)
-                nc.vector.quantize_mx(out=dzt_codes[:].bitcast(E5M2), scales=dzt_scales[:], in_=grouped[:])
-                acc = psum.tile([P, BANK], F32, name="acc", tag="acc")
-                for hp in range(2):
-                    nc.tensor.matmul_mx(
-                        out=acc[:],
-                        lhsT=dzt_codes[:, hp * P : (hp + 1) * P].bitcast(E5M2),
-                        lhsT_scale=dzt_scales[:, hp * P : (hp + 1) * P],
-                        rhs=w_codes[:, hp * BANK : (hp + 1) * BANK].bitcast(E4M3),
-                        rhs_scale=w_scales[:, hp * BANK : (hp + 1) * BANK],
-                        start=(hp == 0), stop=(hp == 1),
-                    )
-                da_copies = keep.tile([P, COPIES * D], F32, name="da%d%d" % (g, j))
-                nc.scalar.copy(
-                    out=da_copies[:].rearrange("p (r n) -> p r n", n=BANK),
-                    in_=acc[:].unsqueeze(1).broadcast_to([P, COPIES // 2, BANK]),
-                )
-                nc.sync.dma_start(out=out0_rows[g, j], in_=da_copies[:].unsqueeze(1).broadcast_to([P, SLOTS // COPIES, COPIES * D]))
-
         h_codes = [keep.tile([P, 2 * D], U32, name="h_codes%d" % g, align_bytes=64) for g in range(PASSES)]
         h_scales = [keep.tile([P, 2 * D], U8, name="h_scales%d" % g, align_bytes=64) for g in range(PASSES)]
         dz_codes = [keep.tile([P, H], U32, name="dz_codes%d" % g, align_bytes=64) for g in range(PASSES)]
         dz_scales = [keep.tile([P, H], U8, name="dz_scales%d" % g, align_bytes=64) for g in range(PASSES)]
+        out0_rows = out_0.rearrange("b s m d -> (b s) (m d)").rearrange("(g p j) (r n) -> g j p r n", p=P, j=PACK, n=COPIES * D)
 
-        for g in range(PASSES):
-            pairs = work.tile([P, 2, 2, P, 2], BF16, name="pairs")
-            for u in range(2):
-                bank = psum.tile([P, BANK], F32, name="sums", tag="sums", bufs=3)
-                for e in range(2):
-                    node = src_sb[g, u][:, e * SLOTS * D : (e + 1) * SLOTS * D]
-                    partial = work.tile([P, SLOTS // 2 * D], F32, name="partial", bufs=3)
-                    nc.vector.tensor_tensor(out=partial[:], in0=node[:, 0 : SLOTS // 2 * D], in1=node[:, SLOTS // 2 * D :], op=ALU.add)
-                    for cc in range(2):
-                        at = (2 * cc + e) * P
-                        for v in range(SLOTS // 2):
-                            nc.tensor.matmul(
-                                bank[:, at : at + P], lhsT=partial[:, v * D + cc * P : v * D + (cc + 1) * P], rhs=ident[:],
-                                is_transpose=True, start=(v == 0), stop=(v == SLOTS // 2 - 1),
-                            )
-                nc.scalar.copy(out=pairs[:, :, u, :, :], in_=bank[:].rearrange("c (cc e w) -> c cc w e", cc=2, e=2))
+        def grouped_tile():
+            return work.tile([P, PACK * D], BF16, name="grouped", bufs=3, align_bytes=64)
+
+        def transpose_bank():
+            return psum.tile([P, BANK], F32, name="transposed")
+
+        def turn_w(hp):
+            words = w_raw[:].bitcast(F32)
+            bank = transpose_bank()
+            for e in range(2):
+                for u in range(2):
+                    first = e * 512 + hp * 256
+                    nc.tensor.transpose(bank[:, (2 * e + u) * P : (2 * e + u + 1) * P], words[:, first + u : first + 256 : 2], ident[:])
+            grouped = grouped_tile()
+            nc.scalar.copy(
+                out=grouped[:].bitcast(F32).rearrange("k (p e u) -> k p e u", e=2, u=2),
+                in_=bank[:].rearrange("k (e u p) -> k p e u", e=2, u=2),
+            )
+            return grouped
+
+        def quantize_w(hp, grouped):
+            for rep in range(2):
+                cols = slice(hp * BANK + rep * D, hp * BANK + (rep + 1) * D)
+                nc.vector.quantize_mx(out=w_codes[:, cols].bitcast(E4M3), scales=w_scales[:, cols], in_=grouped[:])
+
+        def slope_of(i):
+            g, j = divmod(i, PACK)
+            return z_sb[g, j // 2][:, (j % 2) * H : (j % 2 + 1) * H]
+
+        def dz_of(i):
+            g, j = divmod(i, PACK)
+            return dz[g][:, j * H : (j + 1) * H]
+
+        def make_slope(i):
+            nc.vector.tensor_scalar(out=slope_of(i), in0=slope_of(i), scalar1=0.0, scalar2=SLOPE, op0=ALU.is_ge, op1=ALU.max)
+
+        def make_dz(i):
+            nc.vector.tensor_tensor(out=dz_of(i), in0=dz_of(i), in1=slope_of(i), op=ALU.mult)
+
+        def turn_dz(i):
+            words = dz_of(i).bitcast(F32)
+            bank = transpose_bank()
+            for hp in range(2):
+                for u in range(2):
+                    nc.tensor.transpose(bank[:, (2 * hp + u) * P : (2 * hp + u + 1) * P], words[:, hp * 256 + u : (hp + 1) * 256 : 2], ident[:])
+            grouped = grouped_tile()
+            nc.scalar.copy(
+                out=grouped[:].bitcast(F32).rearrange("k (hp r u) -> k hp r u", hp=2, u=2),
+                in_=bank[:].rearrange("k (hp u r) -> k hp r u", hp=2, u=2),
+            )
+            return grouped
+
+        def quantize_turned(i, grouped):
+            dzt_codes = keep.tile([P, 2 * P], U32, name="dzt_codes%d" % i, align_bytes=64)
+            dzt_scales = keep.tile([P, 2 * P], U8, name="dzt_scales%d" % i, align_bytes=64)
+            nc.vector.quantize_mx(out=dzt_codes[:].bitcast(E5M2), scales=dzt_scales[:], in_=grouped[:])
+            return dzt_codes, dzt_scales
+
+        def make_da(i, quantized):
+            g, j = divmod(i, PACK)
+            dzt_codes, dzt_scales = quantized
+            acc = psum.tile([P, BANK], F32, name="acc")
+            for hp in range(2):
+                nc.tensor.matmul_mx(
+                    out=acc[:],
+                    lhsT=dzt_codes[:, hp * P : (hp + 1) * P].bitcast(E5M2),
+                    lhsT_scale=dzt_scales[:, hp * P : (hp + 1) * P],
+                    rhs=w_codes[:, hp * BANK : (hp + 1) * BANK].bitcast(E4M3),
+                    rhs_scale=w_scales[:, hp * BANK : (hp + 1) * BANK],
+                    start=(hp == 0), stop=(hp == 1),
+                )
+            da_copies = keep.tile([P, COPIES * D], F32, name="da%d" % i)
+            nc.scalar.copy(
+                out=da_copies[:].rearrange("p (r n) -> p r n", n=BANK),
+                in_=acc[:].unsqueeze(1).broadcast_to([P, COPIES // 2, BANK]),
+            )
+            nc.sync.dma_start(out=out0_rows[g, j], in_=da_copies[:].unsqueeze(1).broadcast_to([P, SLOTS // COPIES, COPIES * D]))
+
+        def weave_dz(g, n):
+            woven = work.tile([P, BANK * PACK], BF16, name="woven", bufs=3, align_bytes=64)
+            nc.scalar.copy(
+                out=woven[:].rearrange("p (c i t) -> p c t i", i=4, t=PACK),
+                in_=dz[g][:].rearrange("p (t h) -> p t h", t=PACK)[:, :, n * BANK : (n + 1) * BANK].rearrange("p t (c i) -> p c t i", i=4),
+            )
+            return woven
+
+        def quantize_dz(g, n, woven):
+            cols = slice(n * BANK, (n + 1) * BANK)
+            nc.vector.quantize_mx(out=dz_codes[g][:, cols].bitcast(E5M2), scales=dz_scales[g][:, cols], in_=woven[:])
+
+        def sum_src(g, u, pairs):
+            bank = psum.tile([P, BANK], F32, name="sums", bufs=4)
+            for e in range(2):
+                node = src_sb[g, u][:, e * SLOTS * D : (e + 1) * SLOTS * D]
+                partial = work.tile([P, SLOTS // 2 * D], F32, name="partial", bufs=4)
+                nc.vector.tensor_tensor(out=partial[:], in0=node[:, 0 : SLOTS // 2 * D], in1=node[:, SLOTS // 2 * D :], op=ALU.add)
+                for cc in range(2):
+                    at = (2 * cc + e) * P
+                    for v in range(SLOTS // 2):
+                        nc.tensor.matmul(
+                            bank[:, at : at + P], lhsT=partial[:, v * D + cc * P : v * D + (cc + 1) * P], rhs=ident[:],
+                            is_transpose=True, start=(v == 0), stop=(v == SLOTS // 2 - 1),
+                        )
+            nc.scalar.copy(out=pairs[:, :, u, :, :], in_=bank[:].rearrange("c (cc e w) -> c cc w e", cc=2, e=2))
+
+        def turn_src(pairs):
             words = pairs[:].rearrange("c cc u w e -> c (cc u w e)").bitcast(F32)
-            bank = psum.tile([P, BANK], F32, name="tr", tag="tr")
+            bank = transpose_bank()
             for i in range(4):
                 nc.tensor.transpose(bank[:, i * P : (i + 1) * P], words[:, i * P : (i + 1) * P], ident[:])
-            total = work.tile([P, D * PACK], BF16, name="total", tag="grouped", align_bytes=64)
+            grouped = grouped_tile()
             nc.scalar.copy(
-                out=total[:].bitcast(F32).rearrange("p (cc c u) -> p cc c u", cc=2, u=2),
+                out=grouped[:].bitcast(F32).rearrange("p (cc c u) -> p cc c u", cc=2, u=2),
                 in_=bank[:].rearrange("p (cc u c) -> p cc c u", cc=2, u=2),
             )
-            nc.vector.quantize_mx(out=h_codes[g][:, 0:D].bitcast(E4M3), scales=h_scales[g][:, 0:D], in_=total[:])
+            return grouped
 
-            for n in range(2):
-                woven = work.tile([P, BANK * PACK], BF16, name="woven", align_bytes=64)
-                nc.scalar.copy(
-                    out=woven[:].rearrange("p (c i t) -> p c t i", i=4, t=PACK),
-                    in_=dz[g][:].rearrange("p (t h) -> p t h", t=PACK)[:, :, n * BANK : (n + 1) * BANK].rearrange("p t (c i) -> p c t i", i=4),
-                )
-                cols = slice(n * BANK, (n + 1) * BANK)
-                nc.vector.quantize_mx(out=dz_codes[g][:, cols].bitcast(E5M2), scales=dz_scales[g][:, cols], in_=woven[:])
+        def quantize_hidden(g, part, grouped):
+            cols = slice(part * D, (part + 1) * D)
+            nc.vector.quantize_mx(out=h_codes[g][:, cols].bitcast(E4M3), scales=h_scales[g][:, cols], in_=grouped[:])
 
-        for g in range(PASSES):
-            sums_t = work.tile([P, 2, PACK, P], F32, name="sums_t")
+        def sum_neigh(q, sums_t):
+            bank = psum.tile([P, BANK], F32, name="sums", bufs=4)
+            for cc in range(2):
+                for k in range(BLOCKS):
+                    at = cc * CHUNK + k * NODES_PER_BLOCK
+                    for e in range(2):
+                        nc.tensor.matmul(
+                            bank[:, at : at + NODES_PER_BLOCK], lhsT=neigh_sb[q][:, k, e * D + cc * P : e * D + (cc + 1) * P],
+                            rhs=node_of_row[:], start=(e == 0), stop=(e == 1),
+                        )
+            half = q % 2
+            nc.scalar.copy(
+                out=sums_t[:, :, :, half * 64 : (half + 1) * 64],
+                in_=bank[:].rearrange("c (cc p j) -> c cc j p", cc=2, j=PACK),
+            )
+
+        def fold_bits(q):
+            bits = neigh_sb[q][:].rearrange("r k x -> r (k x)").bitcast(I32).rearrange("r (k w) -> r k w", k=2 * BLOCKS)
+            folded = work.tile([P, 2 * BLOCKS, 64], I32, name="folded")
+            nc.vector.tensor_tensor(out=folded[:], in0=bits[:, :, 0:64], in1=bits[:, :, 64:128], op=ALU.bitwise_or)
+            return folded
+
+        def find_peaks(folded):
             peak = work.tile([P, 2 * BLOCKS, 2], F32, name="peak")
+            for width in (32, 16, 8):
+                for half in range(2):
+                    lower = folded[half][:, :, 0:width]
+                    nc.vector.tensor_tensor(out=lower, in0=lower, in1=folded[half][:, :, width : 2 * width], op=ALU.bitwise_or)
+            magnitude = [work.tile([P, 2 * BLOCKS, 8], I32, name="magnitude") for half in range(2)]
             for half in range(2):
-                chunk = neigh_sb[2 * g + half]
-                bank = psum.tile([P, BANK], F32, name="sums", tag="sums", bufs=3)
-                for cc in range(2):
-                    for k in range(BLOCKS):
-                        at = cc * CHUNK + k * NODES_PER_BLOCK
-                        for e in range(2):
-                            nc.tensor.matmul(
-                                bank[:, at : at + NODES_PER_BLOCK], lhsT=chunk[:, k, e * D + cc * P : e * D + (cc + 1) * P],
-                                rhs=node_of_row[:], start=(e == 0), stop=(e == 1),
-                            )
-                nc.scalar.copy(
-                    out=sums_t[:, :, :, half * 64 : (half + 1) * 64],
-                    in_=bank[:].rearrange("c (cc p j) -> c cc j p", cc=2, j=PACK),
-                )
-                bits = chunk[:].rearrange("r k x -> r (k x)").bitcast(I32).rearrange("r (k w) -> r k w", k=2 * BLOCKS)
-                folded = work.tile([P, 2 * BLOCKS, 64], I32, name="folded")
-                nc.vector.tensor_tensor(out=folded[:], in0=bits[:, :, 0:64], in1=bits[:, :, 64:128], op=ALU.bitwise_or)
-                for width in (32, 16, 8):
-                    nc.vector.tensor_tensor(out=folded[:, :, 0:width], in0=folded[:, :, 0:width], in1=folded[:, :, width : 2 * width], op=ALU.bitwise_or)
-                magnitude = work.tile([P, 2 * BLOCKS, 8], I32, name="magnitude")
-                nc.vector.tensor_scalar(out=magnitude[:], in0=folded[:, :, 0:8], scalar1=MAGNITUDE_BITS, scalar2=None, op0=ALU.bitwise_and)
+                nc.vector.tensor_scalar(out=magnitude[half][:], in0=folded[half][:, :, 0:8], scalar1=MAGNITUDE_BITS, scalar2=None, op0=ALU.bitwise_and)
+            for half in range(2):
                 nc.vector.tensor_reduce(
-                    out=peak[:, half * BLOCKS : (half + 1) * BLOCKS, :].rearrange("r k e -> r (k e)"), in_=magnitude[:], axis=AXIS_X, op=ALU.max,
+                    out=peak[:, half * BLOCKS : (half + 1) * BLOCKS, :].rearrange("r k e -> r (k e)"), in_=magnitude[half][:], axis=AXIS_X, op=ALU.max,
                 )
+            return peak
+
+        def count_neigh(peak):
             spread = work.tile([P, 2, 2 * BLOCKS, QUADS], BF16, name="spread")
             for e in range(2):
                 nc.vector.scalar_tensor_tensor(
                     out=spread[:, e], in0=peak[:, :, e : e + 1].broadcast_to([P, 2 * BLOCKS, QUADS]), scalar=0.0,
                     in1=quad_of_row[:].unsqueeze(1).broadcast_to([P, 2 * BLOCKS, QUADS]), op0=ALU.is_gt, op1=ALU.mult,
                 )
-            count = psum.tile([P, PACK], F32, name="count", tag="count", bufs=1)
+            count = psum.tile([P, PACK], F32, name="count", tag="acc")
             for e in range(2):
                 nc.tensor.matmul(count[:], lhsT=spread[:, e].rearrange("r k a -> r (k a)"), rhs=place_of_row[:], start=(e == 0), stop=(e == 1))
+            return count
+
+        def turn_neigh(sums_t):
+            banks = []
+            for cc in range(2):
+                bank = transpose_bank()
+                for j in range(PACK):
+                    nc.tensor.transpose(bank[:, j * P : (j + 1) * P], sums_t[:, cc, j, :], ident[:])
+                banks.append(bank)
+            return banks
+
+        def invert(count):
             divisor = work.tile([P, PACK], F32, name="divisor")
             nc.vector.tensor_scalar(out=divisor[:], in0=count[:], scalar1=MEAN_SCALE, scalar2=None, op0=ALU.max)
             inverse = work.tile([P, PACK], F32, name="inverse")
             nc.vector.reciprocal(out=inverse[:], in_=divisor[:])
-            mean = work.tile([P, D * PACK], BF16, name="mean", tag="grouped", align_bytes=64)
+            return inverse
+
+        def make_mean(banks, inverse):
+            grouped = grouped_tile()
             for cc in range(2):
-                bank = psum.tile([P, BANK], F32, name="tr", tag="tr")
-                for j in range(PACK):
-                    nc.tensor.transpose(bank[:, j * P : (j + 1) * P], sums_t[:, cc, j, :], ident[:])
                 nc.vector.tensor_tensor(
-                    out=mean[:, cc * K_PASS : (cc + 1) * K_PASS].rearrange("p (c j) -> p c j", j=PACK),
-                    in0=bank[:].rearrange("p (j c) -> p c j", j=PACK),
+                    out=grouped[:, cc * K_PASS : (cc + 1) * K_PASS].rearrange("p (c j) -> p c j", j=PACK),
+                    in0=banks[cc][:].rearrange("p (j c) -> p c j", j=PACK),
                     in1=inverse[:].unsqueeze(1).broadcast_to([P, P, PACK]),
                     op=ALU.mult,
                 )
-            nc.vector.quantize_mx(out=h_codes[g][:, D : 2 * D].bitcast(E4M3), scales=h_scales[g][:, D : 2 * D], in_=mean[:])
+            return grouped
 
-        for i, m in enumerate((0, 1, 2, 3)):
+        def dw_pass(acc, m, n, g):
             rows = slice(m * P, (m + 1) * P)
-            dw = keep.tile([P, H], F32, name="dw", tag="z%d%d" % (i // 2, i % 2))
+            cols = slice(n * BANK, (n + 1) * BANK)
+            nc.tensor.matmul_mx(
+                out=acc[:],
+                lhsT=h_codes[g][:, rows].bitcast(E4M3), lhsT_scale=h_scales[g][:, rows],
+                rhs=dz_codes[g][:, cols].bitcast(E5M2), rhs_scale=dz_scales[g][:, cols],
+                start=(g == 0), stop=(g == PASSES - 1),
+            )
+
+        def open_dw(m, tag, bufs):
+            accs = [psum.tile([P, BANK], F32, name="dw_acc", tag=tag, bufs=bufs) for n in range(2)]
             for n in range(2):
-                cols = slice(n * BANK, (n + 1) * BANK)
-                acc = psum.tile([P, BANK], F32, name="acc", tag="acc")
-                for g in range(PASSES):
-                    nc.tensor.matmul_mx(
-                        out=acc[:],
-                        lhsT=h_codes[g][:, rows].bitcast(E4M3), lhsT_scale=h_scales[g][:, rows],
-                        rhs=dz_codes[g][:, cols].bitcast(E5M2), rhs_scale=dz_scales[g][:, cols],
-                        start=(g == 0), stop=(g == PASSES - 1),
-                    )
-                nc.scalar.copy(out=dw[:, cols], in_=acc[:])
-            nc.sync.dma_start(out=out_1[rows, :], in_=dw[:])
+                dw_pass(accs[n], m, n, 0)
+            return accs
+
+        def close_dw(m, accs, second_copy):
+            dw = keep.tile([P, H], F32, name="dw", tag="z%d%d" % (m // 2, m % 2))
+            for n in range(2):
+                dw_pass(accs[n], m, n, 1)
+            nc.scalar.copy(out=dw[:, 0:BANK], in_=accs[0][:])
+            second_copy(out=dw[:, BANK:], in_=accs[1][:])
+            nc.sync.dma_start(out=out_1[m * P : (m + 1) * P, :], in_=dw[:])
+
+        tiles = PASSES * PACK
+        turned, dzt, woven = {}, {}, {}
+        w_grouped = [turn_w(hp) for hp in range(2)]
+        for i in range(tiles):
+            make_slope(i)
+            if i < 2:
+                quantize_w(i, w_grouped[i])
+            else:
+                dzt[i - 2] = quantize_turned(i - 2, turned[i - 2])
+            if 2 <= i < 8:
+                make_da(i - 2, dzt[i - 2])
+            make_dz(i)
+            turned[i] = turn_dz(i)
+
+        pairs = [work.tile([P, 2, 2, P, 2], BF16, name="pairs") for g in range(PASSES)]
+        sums_t = [work.tile([P, 2, PACK, P], F32, name="sums_t") for g in range(PASSES)]
+        for u in range(2):
+            dzt[6 + u] = quantize_turned(6 + u, turned[6 + u])
+            make_da(6 + u, dzt[6 + u])
+            sum_src(0, u, pairs[0])
+        woven[0, 0] = weave_dz(0, 0)
+        sum_src(1, 0, pairs[1])
+        total = [turn_src(pairs[0])]
+        woven[0, 1] = weave_dz(0, 1)
+        sum_src(1, 1, pairs[1])
+        quantize_dz(0, 0, woven[0, 0])
+        sum_neigh(0, sums_t[0])
+        total.append(turn_src(pairs[1]))
+        sum_neigh(1, sums_t[0])
+        woven[1, 0] = weave_dz(1, 0)
+        peak = find_peaks([fold_bits(0), fold_bits(1)])
+        sum_neigh(2, sums_t[1])
+        count = count_neigh(peak)
+        banks = turn_neigh(sums_t[0])
+        sum_neigh(3, sums_t[1])
+        quantize_dz(0, 1, woven[0, 1])
+        woven[1, 1] = weave_dz(1, 1)
+        quantize_hidden(0, 0, total[0])
+        folded = [fold_bits(2), fold_bits(3)]
+        inverse = invert(count)
+        quantize_hidden(1, 0, total[1])
+        mean = make_mean(banks, inverse)
+        banks = turn_neigh(sums_t[1])
+        peak = find_peaks(folded)
+        count = count_neigh(peak)
+        quantize_dz(1, 0, woven[1, 0])
+        quantize_dz(1, 1, woven[1, 1])
+        quantize_hidden(0, 1, mean)
+        inverse = invert(count)
+        close_dw(0, open_dw(0, "sums", 4), nc.scalar.copy)
+        close_dw(1, open_dw(1, "sums", 4), nc.scalar.copy)
+        accs = [open_dw(2, "acc", 2), open_dw(3, "sums", 4)]
+        mean = make_mean(banks, inverse)
+        quantize_hidden(1, 1, mean)
+        for m in range(2, 4):
+            close_dw(m, accs[m - 2], nc.vector.tensor_copy)

@@ -22,11 +22,12 @@ PACK = 4
 K_PASS = P * PACK
 PASSES = T // K_PASS
 BANK = 512
-NODES_PER_BLOCK = 2 * P // SLOTS
-BLOCKS = 8
+NODES_PER_BLOCK = P // 2
+BLOCKS = 4
 CHUNK = BLOCKS * NODES_PER_BLOCK
-QUADS = NODES_PER_BLOCK // PACK
+HALF = SLOTS // 2
 COPIES = 4
+LAG = 3
 SLOPE = 0.01
 MAGNITUDE_BITS = 0x7FFF7FFF
 MEAN_SCALE = 29 / 32
@@ -40,50 +41,41 @@ def tile_syntacticgcn_v_kernel(tc, src, neigh, W_map, b_map, z, grad_out, out_0,
         psum = ctx.enter_context(tc.psum_pool(name="psum", bufs=2))
         ctx.enter_context(tc.manual_schedule())
 
-        z_rows = z.rearrange("(g p j) h -> g p (j h)", p=P, j=PACK)
+        def node_major(tensor):
+            return tensor.rearrange("b s m d -> (b s) (m d)").rearrange("(g p u e) x -> g u p (e x)", p=P, u=2, e=2)
+
+        def load(name, shape, dtype, source):
+            tile = keep.tile(shape, dtype, name=name)
+            nc.sync.dma_start(out=tile[:], in_=source)
+            return tile
+
+        z_rows = z.rearrange("(g p u e) h -> g u p (e h)", p=P, u=2, e=2)
         g_rows = grad_out.rearrange("(g p j) h -> g p (j h)", p=P, j=PACK)
-        w_raw = keep.tile([P, 2 * H], BF16, name="w_raw")
-        z_sb = {}
-        dz = []
-        for g in range(PASSES):
-            g_pass = keep.tile([P, PACK * H], BF16, name="dz%d" % g)
-            dz.append(g_pass)
-            for half in range(2):
-                z_half = keep.tile([P, 2 * H], F32, name="z_half", tag="z%d%d" % (g, half))
-                z_sb[g, half] = z_half
-        nc.sync.dma_start(out=w_raw[:], in_=W_map[0:D, :].rearrange("(p e) h -> p (e h)", e=2))
-        nc.sync.dma_start(out=z_sb[0, 0][:, 0:H], in_=z_rows[0, :, 0:H])
-        nc.sync.dma_start(out=dz[0][:, 0 : 2 * H], in_=g_rows[0, :, 0 : 2 * H])
-        nc.sync.dma_start(out=z_sb[0, 0][:, H : 2 * H], in_=z_rows[0, :, H : 2 * H])
-        for g, half in ((0, 1), (1, 0), (1, 1)):
-            cols = slice(half * 2 * H, (half + 1) * 2 * H)
-            nc.sync.dma_start(out=z_sb[g, half][:], in_=z_rows[g, :, cols])
-            nc.sync.dma_start(out=dz[g][:, cols], in_=g_rows[g, :, cols])
-        src_rows = src.rearrange("b s m d -> (b s) (m d)").rearrange("(g p u e) x -> g u p (e x)", p=P, u=2, e=2)
-        neigh_rows = neigh.rearrange("b s (v e) d -> (b s v) (e d)", e=2).rearrange("(q k r) x -> q r k x", k=BLOCKS, r=P)
-        src_sb, neigh_sb = {}, []
-        for g in range(PASSES):
-            for u in range(2):
-                src_chunk = keep.tile([P, 2 * SLOTS * D], BF16, name="src%d%d" % (g, u))
-                nc.sync.dma_start(out=src_chunk[:], in_=src_rows[g, u])
-                src_sb[g, u] = src_chunk
-        for q in range(T // CHUNK):
-            neigh_chunk = keep.tile([P, BLOCKS, 2 * D], BF16, name="neigh%d" % q)
-            nc.sync.dma_start(out=neigh_chunk[:], in_=neigh_rows[q])
-            neigh_sb.append(neigh_chunk)
+        src_half_rows = src.rearrange("b s (v m) d -> (b s v) (m d)", v=2).rearrange("(q k r) x -> q r k x", k=BLOCKS, r=P)
+        neigh_sb, z_sb, src_sb = {}, {}, {}
+        dz = [keep.tile([P, PACK * H], BF16, name="dz%d" % g) for g in range(PASSES)]
+        neigh_sb[0, 0] = load("neigh00", [P, 2 * SLOTS * D], BF16, node_major(neigh)[0, 0])
+        w_raw = load("w_raw", [P, 2 * H], BF16, W_map[0:D, :].rearrange("(p e) h -> p (e h)", e=2))
+        for u in range(2):
+            z_sb[0, u] = load("z0%d" % u, [P, 2 * H], F32, z_rows[0, u])
+            nc.sync.dma_start(out=dz[0][:, u * 2 * H : (u + 1) * 2 * H], in_=g_rows[0, :, u * 2 * H : (u + 1) * 2 * H])
+        z_sb[1, 0] = load("z10", [P, 2 * H], F32, z_rows[1, 0])
+        nc.sync.dma_start(out=dz[1][:], in_=g_rows[1])
+        z_sb[1, 1] = load("z11", [P, 2 * H], F32, z_rows[1, 1])
+        neigh_sb[0, 1] = load("neigh01", [P, 2 * SLOTS * D], BF16, node_major(neigh)[0, 1])
+        for u in range(2):
+            src_sb[0, u] = load("src0%d" % u, [P, 2 * SLOTS * D], BF16, node_major(src)[0, u])
+        for u in range(2):
+            neigh_sb[1, u] = load("neigh1%d" % u, [P, 2 * SLOTS * D], BF16, node_major(neigh)[1, u])
+        for q in range(2):
+            src_sb[1, q] = load("src1%d" % q, [P, BLOCKS, HALF * D], BF16, src_half_rows[2 + q])
 
         ident = keep.tile([P, P], F32, name="ident")
         make_identity(nc, ident[:])
         node_of_row_f = keep.tile([P, NODES_PER_BLOCK], F32, name="node_of_row_f")
-        nc.vector.tensor_reduce(out=node_of_row_f[:], in_=ident[:].rearrange("p (i v) -> p i v", v=SLOTS // 2), axis=AXIS_X, op=ALU.add)
+        nc.vector.tensor_reduce(out=node_of_row_f[:], in_=ident[:].rearrange("p (i v) -> p i v", v=2), axis=AXIS_X, op=ALU.add)
         node_of_row = keep.tile([P, NODES_PER_BLOCK], BF16, name="node_of_row")
-        nc.vector.tensor_scalar(out=node_of_row[:], in0=node_of_row_f[:], scalar1=MEAN_SCALE, scalar2=None, op0=ALU.mult)
-        quad_of_row = keep.tile([P, QUADS], F32, name="quad_of_row")
-        nc.vector.tensor_reduce(out=quad_of_row[:], in_=node_of_row_f[:].rearrange("p (a j) -> p a j", j=PACK), axis=AXIS_X, op=ALU.add)
-        place_of_row_f = keep.tile([P, PACK], F32, name="place_of_row_f")
-        nc.vector.tensor_reduce(out=place_of_row_f[:], in_=node_of_row_f[:].rearrange("p (a j) -> p j a", j=PACK), axis=AXIS_X, op=ALU.add)
-        place_of_row = keep.tile([P, PACK], BF16, name="place_of_row")
-        nc.vector.tensor_scalar(out=place_of_row[:], in0=place_of_row_f[:], scalar1=MEAN_SCALE, scalar2=None, op0=ALU.mult)
+        nc.vector.tensor_copy(out=node_of_row[:], in_=node_of_row_f[:])
 
         w_codes = keep.tile([P, 2 * BANK], U32, name="w_codes", align_bytes=64)
         w_scales = keep.tile([P, 2 * BANK], U8, name="w_scales", align_bytes=64)
@@ -94,7 +86,7 @@ def tile_syntacticgcn_v_kernel(tc, src, neigh, W_map, b_map, z, grad_out, out_0,
         out0_rows = out_0.rearrange("b s m d -> (b s) (m d)").rearrange("(g p j) (r n) -> g j p r n", p=P, j=PACK, n=COPIES * D)
 
         def grouped_tile():
-            return work.tile([P, PACK * D], BF16, name="grouped", bufs=3, align_bytes=64)
+            return work.tile([P, PACK * D], BF16, name="grouped", bufs=4, align_bytes=64)
 
         def transpose_bank():
             return psum.tile([P, BANK], F32, name="transposed")
@@ -172,7 +164,7 @@ def tile_syntacticgcn_v_kernel(tc, src, neigh, W_map, b_map, z, grad_out, out_0,
             nc.sync.dma_start(out=out0_rows[g, j], in_=da_copies[:].unsqueeze(1).broadcast_to([P, SLOTS // COPIES, COPIES * D]))
 
         def weave_dz(g, n):
-            woven = work.tile([P, BANK * PACK], BF16, name="woven", bufs=3, align_bytes=64)
+            woven = work.tile([P, BANK * PACK], BF16, name="woven", bufs=2, align_bytes=64)
             nc.scalar.copy(
                 out=woven[:].rearrange("p (c i t) -> p c t i", i=4, t=PACK),
                 in_=dz[g][:].rearrange("p (t h) -> p t h", t=PACK)[:, :, n * BANK : (n + 1) * BANK].rearrange("p t (c i) -> p c t i", i=4),
@@ -183,20 +175,54 @@ def tile_syntacticgcn_v_kernel(tc, src, neigh, W_map, b_map, z, grad_out, out_0,
             cols = slice(n * BANK, (n + 1) * BANK)
             nc.vector.quantize_mx(out=dz_codes[g][:, cols].bitcast(E5M2), scales=dz_scales[g][:, cols], in_=woven[:])
 
-        def sum_src(g, u, pairs):
-            bank = psum.tile([P, BANK], F32, name="sums", bufs=4)
+        def add_turned(bank, e, partials):
+            for cc in range(2):
+                at = (2 * cc + e) * P
+                parts = [part[:, v * D + cc * P : v * D + (cc + 1) * P] for part in partials for v in range(HALF)]
+                for n, part in enumerate(parts):
+                    nc.tensor.matmul(bank[:, at : at + P], lhsT=part, rhs=ident[:], is_transpose=True, start=(n == 0), stop=(n == len(parts) - 1))
+
+        def partial_tile():
+            return work.tile([P, HALF * D], F32, name="partial", bufs=4)
+
+        def sums_bank():
+            return psum.tile([P, BANK], F32, name="sums", bufs=4)
+
+        def slot_halves(chunk, e):
+            return [chunk[:, (2 * e + v) * HALF * D : (2 * e + v + 1) * HALF * D] for v in range(2)]
+
+        def widen_slots(chunk, e):
+            partials = [partial_tile(), partial_tile()]
+            for partial, half in zip(partials, slot_halves(chunk, e)):
+                nc.scalar.copy(out=partial[:], in_=half)
+            return partials
+
+        def sum_slots(chunk):
+            bank = sums_bank()
             for e in range(2):
-                node = src_sb[g, u][:, e * SLOTS * D : (e + 1) * SLOTS * D]
-                partial = work.tile([P, SLOTS // 2 * D], F32, name="partial", bufs=4)
-                nc.vector.tensor_tensor(out=partial[:], in0=node[:, 0 : SLOTS // 2 * D], in1=node[:, SLOTS // 2 * D :], op=ALU.add)
-                for cc in range(2):
-                    at = (2 * cc + e) * P
-                    for v in range(SLOTS // 2):
-                        nc.tensor.matmul(
-                            bank[:, at : at + P], lhsT=partial[:, v * D + cc * P : v * D + (cc + 1) * P], rhs=ident[:],
-                            is_transpose=True, start=(v == 0), stop=(v == SLOTS // 2 - 1),
-                        )
+                partial = partial_tile()
+                lower, upper = slot_halves(chunk, e)
+                nc.vector.tensor_tensor(out=partial[:], in0=lower, in1=upper, op=ALU.add)
+                add_turned(bank, e, [partial])
+            return bank
+
+        def pair_src(u, bank, pairs):
             nc.scalar.copy(out=pairs[:, :, u, :, :], in_=bank[:].rearrange("c (cc e w) -> c cc w e", cc=2, e=2))
+
+        def sum_src_rows(q, pairs):
+            bank = sums_bank()
+            for cc in range(2):
+                for k in range(BLOCKS):
+                    at = cc * CHUNK + k * NODES_PER_BLOCK
+                    for m in range(HALF):
+                        nc.tensor.matmul(
+                            bank[:, at : at + NODES_PER_BLOCK], lhsT=src_sb[1, q][:, k, m * D + cc * P : m * D + (cc + 1) * P],
+                            rhs=node_of_row[:], start=(m == 0), stop=(m == HALF - 1),
+                        )
+            nc.scalar.copy(
+                out=pairs[:, :, :, q * 64 : (q + 1) * 64, :],
+                in_=bank[:].rearrange("c (cc w u e) -> c cc u w e", cc=2, u=2, e=2),
+            )
 
         def turn_src(pairs):
             words = pairs[:].rearrange("c cc u w e -> c (cc u w e)").bitcast(F32)
@@ -214,78 +240,59 @@ def tile_syntacticgcn_v_kernel(tc, src, neigh, W_map, b_map, z, grad_out, out_0,
             cols = slice(part * D, (part + 1) * D)
             nc.vector.quantize_mx(out=h_codes[g][:, cols].bitcast(E4M3), scales=h_scales[g][:, cols], in_=grouped[:])
 
-        def sum_neigh(q, sums_t):
-            bank = psum.tile([P, BANK], F32, name="sums", bufs=4)
-            for cc in range(2):
-                for k in range(BLOCKS):
-                    at = cc * CHUNK + k * NODES_PER_BLOCK
-                    for e in range(2):
-                        nc.tensor.matmul(
-                            bank[:, at : at + NODES_PER_BLOCK], lhsT=neigh_sb[q][:, k, e * D + cc * P : e * D + (cc + 1) * P],
-                            rhs=node_of_row[:], start=(e == 0), stop=(e == 1),
-                        )
-            half = q % 2
-            nc.scalar.copy(
-                out=sums_t[:, :, :, half * 64 : (half + 1) * 64],
-                in_=bank[:].rearrange("c (cc p j) -> c cc j p", cc=2, j=PACK),
+        def keep_neigh(u, bank, sums_t):
+            nc.scalar.activation(
+                out=sums_t[:, :, 2 * u * P : 2 * (u + 1) * P], in_=bank[:].rearrange("c (cc x) -> c cc x", cc=2),
+                func=mybir.ActivationFunctionType.Copy, scale=MEAN_SCALE,
             )
 
-        def fold_bits(q):
-            bits = neigh_sb[q][:].rearrange("r k x -> r (k x)").bitcast(I32).rearrange("r (k w) -> r k w", k=2 * BLOCKS)
-            folded = work.tile([P, 2 * BLOCKS, 64], I32, name="folded")
-            nc.vector.tensor_tensor(out=folded[:], in0=bits[:, :, 0:64], in1=bits[:, :, 64:128], op=ALU.bitwise_or)
-            return folded
-
-        def find_peaks(folded):
-            peak = work.tile([P, 2 * BLOCKS, 2], F32, name="peak")
+        def find_peaks(chunks, peak):
+            folded, magnitude = {}, {}
+            for key in chunks:
+                bits = neigh_sb[key][:].bitcast(I32).rearrange("p (k w) -> p k w", k=2 * SLOTS)
+                folded[key] = work.tile([P, 2 * SLOTS, 64], I32, name="folded", bufs=3)
+                nc.vector.tensor_tensor(out=folded[key][:], in0=bits[:, :, 0:64], in1=bits[:, :, 64:128], op=ALU.bitwise_or)
             for width in (32, 16, 8):
-                for half in range(2):
-                    lower = folded[half][:, :, 0:width]
-                    nc.vector.tensor_tensor(out=lower, in0=lower, in1=folded[half][:, :, width : 2 * width], op=ALU.bitwise_or)
-            magnitude = [work.tile([P, 2 * BLOCKS, 8], I32, name="magnitude") for half in range(2)]
-            for half in range(2):
-                nc.vector.tensor_scalar(out=magnitude[half][:], in0=folded[half][:, :, 0:8], scalar1=MAGNITUDE_BITS, scalar2=None, op0=ALU.bitwise_and)
-            for half in range(2):
-                nc.vector.tensor_reduce(
-                    out=peak[:, half * BLOCKS : (half + 1) * BLOCKS, :].rearrange("r k e -> r (k e)"), in_=magnitude[half][:], axis=AXIS_X, op=ALU.max,
-                )
-            return peak
+                for key in chunks:
+                    lower = folded[key][:, :, 0:width]
+                    nc.vector.tensor_tensor(out=lower, in0=lower, in1=folded[key][:, :, width : 2 * width], op=ALU.bitwise_or)
+            for key in chunks:
+                magnitude[key] = work.tile([P, 2 * SLOTS, 8], I32, name="magnitude", bufs=3)
+                nc.vector.tensor_scalar(out=magnitude[key][:], in0=folded[key][:, :, 0:8], scalar1=MAGNITUDE_BITS, scalar2=None, op0=ALU.bitwise_and)
+            for g, u in chunks:
+                at = (2 * g + u) * 2 * SLOTS
+                nc.vector.tensor_reduce(out=peak[:, at : at + 2 * SLOTS], in_=magnitude[g, u][:], axis=AXIS_X, op=ALU.max)
 
-        def count_neigh(peak):
-            spread = work.tile([P, 2, 2 * BLOCKS, QUADS], BF16, name="spread")
-            for e in range(2):
-                nc.vector.scalar_tensor_tensor(
-                    out=spread[:, e], in0=peak[:, :, e : e + 1].broadcast_to([P, 2 * BLOCKS, QUADS]), scalar=0.0,
-                    in1=quad_of_row[:].unsqueeze(1).broadcast_to([P, 2 * BLOCKS, QUADS]), op0=ALU.is_gt, op1=ALU.mult,
-                )
-            count = psum.tile([P, PACK], F32, name="count", tag="acc")
-            for e in range(2):
-                nc.tensor.matmul(count[:], lhsT=spread[:, e].rearrange("r k a -> r (k a)"), rhs=place_of_row[:], start=(e == 0), stop=(e == 1))
-            return count
-
-        def turn_neigh(sums_t):
+        def turn_neigh(sums_t, new_bank):
             banks = []
             for cc in range(2):
-                bank = transpose_bank()
+                bank = new_bank()
                 for j in range(PACK):
-                    nc.tensor.transpose(bank[:, j * P : (j + 1) * P], sums_t[:, cc, j, :], ident[:])
+                    nc.tensor.transpose(bank[:, j * P : (j + 1) * P], sums_t[:, cc, j * P : (j + 1) * P], ident[:])
                 banks.append(bank)
             return banks
 
+        def count_slots(peak):
+            present = keep.tile([P, PASSES * PACK * SLOTS], F32, name="present")
+            nc.vector.tensor_scalar(out=present[:], in0=peak[:], scalar1=0.0, scalar2=MEAN_SCALE, op0=ALU.is_gt, op1=ALU.mult)
+            count = keep.tile([P, PASSES * PACK], F32, name="count")
+            nc.vector.tensor_reduce(out=count[:], in_=present[:].rearrange("p (j m) -> p j m", m=SLOTS), axis=AXIS_X, op=ALU.add)
+            return count
+
         def invert(count):
-            divisor = work.tile([P, PACK], F32, name="divisor")
+            divisor = keep.tile([P, PASSES * PACK], F32, name="divisor")
             nc.vector.tensor_scalar(out=divisor[:], in0=count[:], scalar1=MEAN_SCALE, scalar2=None, op0=ALU.max)
-            inverse = work.tile([P, PACK], F32, name="inverse")
+            inverse = keep.tile([P, PASSES * PACK], F32, name="inverse")
             nc.vector.reciprocal(out=inverse[:], in_=divisor[:])
             return inverse
 
-        def make_mean(banks, inverse):
+        def make_mean(g, banks, inverse):
             grouped = grouped_tile()
             for cc in range(2):
                 nc.vector.tensor_tensor(
                     out=grouped[:, cc * K_PASS : (cc + 1) * K_PASS].rearrange("p (c j) -> p c j", j=PACK),
                     in0=banks[cc][:].rearrange("p (j c) -> p c j", j=PACK),
-                    in1=inverse[:].unsqueeze(1).broadcast_to([P, P, PACK]),
+                    in1=inverse[:, g * PACK : (g + 1) * PACK].unsqueeze(1).broadcast_to([P, P, PACK]),
                     op=ALU.mult,
                 )
             return grouped
@@ -314,59 +321,63 @@ def tile_syntacticgcn_v_kernel(tc, src, neigh, W_map, b_map, z, grad_out, out_0,
             second_copy(out=dw[:, BANK:], in_=accs[1][:])
             nc.sync.dma_start(out=out_1[m * P : (m + 1) * P, :], in_=dw[:])
 
+        pairs = [work.tile([P, 2, 2, P, 2], BF16, name="pairs") for g in range(PASSES)]
+        sums_t = [work.tile([P, 2, PACK * P], F32, name="sums_t") for g in range(PASSES)]
+        peak = keep.tile([P, PASSES * PACK * SLOTS], F32, name="peak")
         tiles = PASSES * PACK
         turned, dzt, woven = {}, {}, {}
+        find_peaks([(0, 0)], peak)
+        partials = widen_slots(neigh_sb[0, 0], 0)
         w_grouped = [turn_w(hp) for hp in range(2)]
+        first_bank = sums_bank()
+        add_turned(first_bank, 0, partials)
+        partials = widen_slots(neigh_sb[0, 0], 1)
         for i in range(tiles):
             make_slope(i)
             if i < 2:
                 quantize_w(i, w_grouped[i])
-            else:
-                dzt[i - 2] = quantize_turned(i - 2, turned[i - 2])
-            if 2 <= i < 8:
-                make_da(i - 2, dzt[i - 2])
+            elif i >= LAG:
+                make_da(i - LAG, quantize_turned(i - LAG, turned[i - LAG]))
             make_dz(i)
             turned[i] = turn_dz(i)
+            if i == 0:
+                add_turned(first_bank, 1, partials)
+                keep_neigh(0, first_bank, sums_t[0])
 
-        pairs = [work.tile([P, 2, 2, P, 2], BF16, name="pairs") for g in range(PASSES)]
-        sums_t = [work.tile([P, 2, PACK, P], F32, name="sums_t") for g in range(PASSES)]
-        for u in range(2):
-            dzt[6 + u] = quantize_turned(6 + u, turned[6 + u])
-            make_da(6 + u, dzt[6 + u])
-            sum_src(0, u, pairs[0])
+        make_da(5, quantize_turned(5, turned[5]))
+        bank = sum_slots(neigh_sb[0, 1])
+        make_da(6, quantize_turned(6, turned[6]))
+        keep_neigh(1, bank, sums_t[0])
+        make_da(7, quantize_turned(7, turned[7]))
+        pair_src(0, sum_slots(src_sb[0, 0]), pairs[0])
         woven[0, 0] = weave_dz(0, 0)
-        sum_src(1, 0, pairs[1])
-        total = [turn_src(pairs[0])]
+        pair_src(1, sum_slots(src_sb[0, 1]), pairs[0])
         woven[0, 1] = weave_dz(0, 1)
-        sum_src(1, 1, pairs[1])
+        bank = sum_slots(neigh_sb[1, 0])
+        total = [turn_src(pairs[0])]
+        keep_neigh(0, bank, sums_t[1])
+        sum_src_rows(0, pairs[1])
+        bank = sum_slots(neigh_sb[1, 1])
         quantize_dz(0, 0, woven[0, 0])
-        sum_neigh(0, sums_t[0])
-        total.append(turn_src(pairs[1]))
-        sum_neigh(1, sums_t[0])
         woven[1, 0] = weave_dz(1, 0)
-        peak = find_peaks([fold_bits(0), fold_bits(1)])
-        sum_neigh(2, sums_t[1])
-        count = count_neigh(peak)
-        banks = turn_neigh(sums_t[0])
-        sum_neigh(3, sums_t[1])
+        keep_neigh(1, bank, sums_t[1])
         quantize_dz(0, 1, woven[0, 1])
+        sum_src_rows(1, pairs[1])
         woven[1, 1] = weave_dz(1, 1)
+        banks = [turn_neigh(sums_t[0], sums_bank)]
+        total.append(turn_src(pairs[1]))
+        banks.append(turn_neigh(sums_t[1], sums_bank))
         quantize_hidden(0, 0, total[0])
-        folded = [fold_bits(2), fold_bits(3)]
-        inverse = invert(count)
-        quantize_hidden(1, 0, total[1])
-        mean = make_mean(banks, inverse)
-        banks = turn_neigh(sums_t[1])
-        peak = find_peaks(folded)
-        count = count_neigh(peak)
+        find_peaks([(0, 1), (1, 0), (1, 1)], peak)
         quantize_dz(1, 0, woven[1, 0])
         quantize_dz(1, 1, woven[1, 1])
-        quantize_hidden(0, 1, mean)
+        count = count_slots(peak)
+        quantize_hidden(1, 0, total[1])
+        close_dw(0, open_dw(0, "acc", 2), nc.scalar.copy)
+        close_dw(1, open_dw(1, "transposed", 2), nc.scalar.copy)
         inverse = invert(count)
-        close_dw(0, open_dw(0, "sums", 4), nc.scalar.copy)
-        close_dw(1, open_dw(1, "sums", 4), nc.scalar.copy)
-        accs = [open_dw(2, "acc", 2), open_dw(3, "sums", 4)]
-        mean = make_mean(banks, inverse)
-        quantize_hidden(1, 1, mean)
+        quantize_hidden(0, 1, make_mean(0, banks[0], inverse))
+        accs = [open_dw(2, "acc", 2), open_dw(3, "transposed", 2)]
+        quantize_hidden(1, 1, make_mean(1, banks[1], inverse))
         for m in range(2, 4):
             close_dw(m, accs[m - 2], nc.vector.tensor_copy)

from contextlib import ExitStack

import concourse.mybir as mybir
from concourse.masks import make_identity

T, SLOTS, D, H = 1024, 8, 256, 1024
FLOPS = 2 * T * H * D + 2 * T * 2 * D * H
BYTES = 2 * (T * SLOTS * D * 2) + D * H * 2 + T * H * 4 + T * H * 2 + T * SLOTS * D * 4 + 2 * D * H * 4

F32 = mybir.dt.float32
BF16 = mybir.dt.bfloat16
I32 = mybir.dt.int32
U32 = mybir.dt.uint32
U8 = mybir.dt.uint8
E4M3 = mybir.dt.float8_e4m3fn_x4
E5M2 = mybir.dt.float8_e5m2_x4
ALU = mybir.AluOpType
AXIS_X = mybir.AxisListType.X

P = 128
PACK = 4
K_PASS = P * PACK
PASSES = T // K_PASS
BANK = 512
NODES_PER_BLOCK = P // 2
BLOCKS = 4
CHUNK = BLOCKS * NODES_PER_BLOCK
HALF = SLOTS // 2
COPIES = 4
LAG = 3
SLOPE = 0.01
MAGNITUDE_BITS = 0x7FFF7FFF
MEAN_SCALE = 29 / 32


def tile_syntacticgcn_v_kernel(tc, src, neigh, W_map, b_map, z, grad_out, out_0, out_1):
    nc = tc.nc
    with ExitStack() as ctx:
        keep = ctx.enter_context(tc.tile_pool(name="keep", bufs=1))
        work = ctx.enter_context(tc.tile_pool(name="work", bufs=2))
        psum = ctx.enter_context(tc.psum_pool(name="psum", bufs=2))
        ctx.enter_context(tc.manual_schedule())

        def node_major(tensor):
            return tensor.rearrange("b s m d -> (b s) (m d)").rearrange("(g p u e) x -> g u p (e x)", p=P, u=2, e=2)

        def load(name, shape, dtype, source):
            tile = keep.tile(shape, dtype, name=name)
            nc.sync.dma_start(out=tile[:], in_=source)
            return tile

        z_rows = z.rearrange("(g p u e) h -> g u p (e h)", p=P, u=2, e=2)
        g_rows = grad_out.rearrange("(g p j) h -> g p (j h)", p=P, j=PACK)
        src_half_rows = src.rearrange("b s (v m) d -> (b s v) (m d)", v=2).rearrange("(q k r) x -> q r k x", k=BLOCKS, r=P)
        neigh_sb, z_sb, src_sb = {}, {}, {}
        dz = [keep.tile([P, PACK * H], BF16, name="dz%d" % g) for g in range(PASSES)]
        neigh_sb[0, 0] = load("neigh00", [P, 2 * SLOTS * D], BF16, node_major(neigh)[0, 0])
        w_raw = load("w_raw", [P, 2 * H], BF16, W_map[0:D, :].rearrange("(p e) h -> p (e h)", e=2))
        for u in range(2):
            z_sb[0, u] = load("z0%d" % u, [P, 2 * H], F32, z_rows[0, u])
            nc.sync.dma_start(out=dz[0][:, u * 2 * H : (u + 1) * 2 * H], in_=g_rows[0, :, u * 2 * H : (u + 1) * 2 * H])
        z_sb[1, 0] = load("z10", [P, 2 * H], F32, z_rows[1, 0])
        nc.sync.dma_start(out=dz[1][:], in_=g_rows[1])
        z_sb[1, 1] = load("z11", [P, 2 * H], F32, z_rows[1, 1])
        neigh_sb[0, 1] = load("neigh01", [P, 2 * SLOTS * D], BF16, node_major(neigh)[0, 1])
        for u in range(2):
            src_sb[0, u] = load("src0%d" % u, [P, 2 * SLOTS * D], BF16, node_major(src)[0, u])
        for u in range(2):
            neigh_sb[1, u] = load("neigh1%d" % u, [P, 2 * SLOTS * D], BF16, node_major(neigh)[1, u])
        for q in range(2):
            src_sb[1, q] = load("src1%d" % q, [P, BLOCKS, HALF * D], BF16, src_half_rows[2 + q])

        ident = keep.tile([P, P], F32, name="ident")
        make_identity(nc, ident[:])
        node_of_row_f = keep.tile([P, NODES_PER_BLOCK], F32, name="node_of_row_f")
        nc.vector.tensor_reduce(out=node_of_row_f[:], in_=ident[:].rearrange("p (i v) -> p i v", v=2), axis=AXIS_X, op=ALU.add)
        node_of_row = keep.tile([P, NODES_PER_BLOCK], BF16, name="node_of_row")
        nc.vector.tensor_copy(out=node_of_row[:], in_=node_of_row_f[:])

        w_codes = keep.tile([P, 2 * BANK], U32, name="w_codes", align_bytes=64)
        w_scales = keep.tile([P, 2 * BANK], U8, name="w_scales", align_bytes=64)
        h_codes = [keep.tile([P, 2 * D], U32, name="h_codes%d" % g, align_bytes=64) for g in range(PASSES)]
        h_scales = [keep.tile([P, 2 * D], U8, name="h_scales%d" % g, align_bytes=64) for g in range(PASSES)]
        dz_codes = [keep.tile([P, H], U32, name="dz_codes%d" % g, align_bytes=64) for g in range(PASSES)]
        dz_scales = [keep.tile([P, H], U8, name="dz_scales%d" % g, align_bytes=64) for g in range(PASSES)]
        out0_rows = out_0.rearrange("b s m d -> (b s) (m d)").rearrange("(g p j) (r n) -> g j p r n", p=P, j=PACK, n=COPIES * D)

        def grouped_tile():
            return work.tile([P, PACK * D], BF16, name="grouped", bufs=4, align_bytes=64)

        def transpose_bank():
            return psum.tile([P, BANK], F32, name="transposed")

        def turn_w(hp):
            words = w_raw[:].bitcast(F32)
            bank = transpose_bank()
            for e in range(2):
                for u in range(2):
                    first = e * 512 + hp * 256
                    nc.tensor.transpose(bank[:, (2 * e + u) * P : (2 * e + u + 1) * P], words[:, first + u : first + 256 : 2], ident[:])
            grouped = grouped_tile()
            nc.scalar.copy(
                out=grouped[:].bitcast(F32).rearrange("k (p e u) -> k p e u", e=2, u=2),
                in_=bank[:].rearrange("k (e u p) -> k p e u", e=2, u=2),
            )
            return grouped

        def quantize_w(hp, grouped):
            for rep in range(2):
                cols = slice(hp * BANK + rep * D, hp * BANK + (rep + 1) * D)
                nc.vector.quantize_mx(out=w_codes[:, cols].bitcast(E4M3), scales=w_scales[:, cols], in_=grouped[:])

        def slope_of(i):
            g, j = divmod(i, PACK)
            return z_sb[g, j // 2][:, (j % 2) * H : (j % 2 + 1) * H]

        def dz_of(i):
            g, j = divmod(i, PACK)
            return dz[g][:, j * H : (j + 1) * H]

        def make_slope(i):
            nc.vector.tensor_scalar(out=slope_of(i), in0=slope_of(i), scalar1=0.0, scalar2=SLOPE, op0=ALU.is_ge, op1=ALU.max)

        def make_dz(i):
            nc.vector.tensor_tensor(out=dz_of(i), in0=dz_of(i), in1=slope_of(i), op=ALU.mult)

        def turn_dz(i):
            words = dz_of(i).bitcast(F32)
            bank = transpose_bank()
            for hp in range(2):
                for u in range(2):
                    nc.tensor.transpose(bank[:, (2 * hp + u) * P : (2 * hp + u + 1) * P], words[:, hp * 256 + u : (hp + 1) * 256 : 2], ident[:])
            grouped = grouped_tile()
            nc.scalar.copy(
                out=grouped[:].bitcast(F32).rearrange("k (hp r u) -> k hp r u", hp=2, u=2),
                in_=bank[:].rearrange("k (hp u r) -> k hp r u", hp=2, u=2),
            )
            return grouped

        def quantize_turned(i, grouped):
            dzt_codes = keep.tile([P, 2 * P], U32, name="dzt_codes%d" % i, align_bytes=64)
            dzt_scales = keep.tile([P, 2 * P], U8, name="dzt_scales%d" % i, align_bytes=64)
            nc.vector.quantize_mx(out=dzt_codes[:].bitcast(E5M2), scales=dzt_scales[:], in_=grouped[:])
            return dzt_codes, dzt_scales

        def make_da(i, quantized):
            g, j = divmod(i, PACK)
            dzt_codes, dzt_scales = quantized
            acc = psum.tile([P, BANK], F32, name="acc")
            for hp in range(2):
                nc.tensor.matmul_mx(
                    out=acc[:],
                    lhsT=dzt_codes[:, hp * P : (hp + 1) * P].bitcast(E5M2),
                    lhsT_scale=dzt_scales[:, hp * P : (hp + 1) * P],
                    rhs=w_codes[:, hp * BANK : (hp + 1) * BANK].bitcast(E4M3),
                    rhs_scale=w_scales[:, hp * BANK : (hp + 1) * BANK],
                    start=(hp == 0), stop=(hp == 1),
                )
            da_copies = keep.tile([P, COPIES * D], F32, name="da%d" % i)
            nc.scalar.copy(
                out=da_copies[:].rearrange("p (r n) -> p r n", n=BANK),
                in_=acc[:].unsqueeze(1).broadcast_to([P, COPIES // 2, BANK]),
            )
            nc.sync.dma_start(out=out0_rows[g, j], in_=da_copies[:].unsqueeze(1).broadcast_to([P, SLOTS // COPIES, COPIES * D]))

        def weave_dz(g, n):
            woven = work.tile([P, BANK * PACK], BF16, name="woven", bufs=2, align_bytes=64)
            nc.scalar.copy(
                out=woven[:].rearrange("p (c i t) -> p c t i", i=4, t=PACK),
                in_=dz[g][:].rearrange("p (t h) -> p t h", t=PACK)[:, :, n * BANK : (n + 1) * BANK].rearrange("p t (c i) -> p c t i", i=4),
            )
            return woven

        def quantize_dz(g, n, woven):
            cols = slice(n * BANK, (n + 1) * BANK)
            nc.vector.quantize_mx(out=dz_codes[g][:, cols].bitcast(E5M2), scales=dz_scales[g][:, cols], in_=woven[:])

        def add_turned(bank, e, partials):
            for cc in range(2):
                at = (2 * cc + e) * P
                parts = [part[:, v * D + cc * P : v * D + (cc + 1) * P] for part in partials for v in range(HALF)]
                for n, part in enumerate(parts):
                    nc.tensor.matmul(bank[:, at : at + P], lhsT=part, rhs=ident[:], is_transpose=True, start=(n == 0), stop=(n == len(parts) - 1))

        def partial_tile():
            return work.tile([P, HALF * D], F32, name="partial", bufs=4)

        def sums_bank():
            return psum.tile([P, BANK], F32, name="sums", bufs=4)

        def slot_halves(chunk, e):
            return [chunk[:, (2 * e + v) * HALF * D : (2 * e + v + 1) * HALF * D] for v in range(2)]

        def widen_slots(chunk, e):
            partials = [partial_tile(), partial_tile()]
            for partial, half in zip(partials, slot_halves(chunk, e)):
                nc.scalar.copy(out=partial[:], in_=half)
            return partials

        def sum_slots(chunk):
            bank = sums_bank()
            for e in range(2):
                partial = partial_tile()
                lower, upper = slot_halves(chunk, e)
                nc.vector.tensor_tensor(out=partial[:], in0=lower, in1=upper, op=ALU.add)
                add_turned(bank, e, [partial])
            return bank

        def pair_src(u, bank, pairs):
            nc.scalar.copy(out=pairs[:, :, u, :, :], in_=bank[:].rearrange("c (cc e w) -> c cc w e", cc=2, e=2))

        def sum_src_rows(q, pairs):
            bank = sums_bank()
            for cc in range(2):
                for k in range(BLOCKS):
                    at = cc * CHUNK + k * NODES_PER_BLOCK
                    for m in range(HALF):
                        nc.tensor.matmul(
                            bank[:, at : at + NODES_PER_BLOCK], lhsT=src_sb[1, q][:, k, m * D + cc * P : m * D + (cc + 1) * P],
                            rhs=node_of_row[:], start=(m == 0), stop=(m == HALF - 1),
                        )
            nc.scalar.copy(
                out=pairs[:, :, :, q * 64 : (q + 1) * 64, :],
                in_=bank[:].rearrange("c (cc w u e) -> c cc u w e", cc=2, u=2, e=2),
            )

        def turn_src(pairs):
            words = pairs[:].rearrange("c cc u w e -> c (cc u w e)").bitcast(F32)
            bank = transpose_bank()
            for i in range(4):
                nc.tensor.transpose(bank[:, i * P : (i + 1) * P], words[:, i * P : (i + 1) * P], ident[:])
            grouped = grouped_tile()
            nc.scalar.copy(
                out=grouped[:].bitcast(F32).rearrange("p (cc c u) -> p cc c u", cc=2, u=2),
                in_=bank[:].rearrange("p (cc u c) -> p cc c u", cc=2, u=2),
            )
            return grouped

        def quantize_hidden(g, part, grouped):
            cols = slice(part * D, (part + 1) * D)
            nc.vector.quantize_mx(out=h_codes[g][:, cols].bitcast(E4M3), scales=h_scales[g][:, cols], in_=grouped[:])

        def keep_neigh(u, bank, sums_t):
            nc.scalar.activation(
                out=sums_t[:, :, 2 * u * P : 2 * (u + 1) * P], in_=bank[:].rearrange("c (cc x) -> c cc x", cc=2),
                func=mybir.ActivationFunctionType.Copy, scale=MEAN_SCALE,
            )

        def find_peaks(chunks, peak):
            folded, magnitude = {}, {}
            for key in chunks:
                bits = neigh_sb[key][:].bitcast(I32).rearrange("p (k w) -> p k w", k=2 * SLOTS)
                folded[key] = work.tile([P, 2 * SLOTS, 64], I32, name="folded", bufs=3)
                nc.vector.tensor_tensor(out=folded[key][:], in0=bits[:, :, 0:64], in1=bits[:, :, 64:128], op=ALU.bitwise_or)
            for width in (32, 16, 8):
                for key in chunks:
                    lower = folded[key][:, :, 0:width]
                    nc.vector.tensor_tensor(out=lower, in0=lower, in1=folded[key][:, :, width : 2 * width], op=ALU.bitwise_or)
            for key in chunks:
                magnitude[key] = work.tile([P, 2 * SLOTS, 8], I32, name="magnitude", bufs=3)
                nc.vector.tensor_scalar(out=magnitude[key][:], in0=folded[key][:, :, 0:8], scalar1=MAGNITUDE_BITS, scalar2=None, op0=ALU.bitwise_and)
            for g, u in chunks:
                at = (2 * g + u) * 2 * SLOTS
                nc.vector.tensor_reduce(out=peak[:, at : at + 2 * SLOTS], in_=magnitude[g, u][:], axis=AXIS_X, op=ALU.max)

        def turn_neigh(sums_t, new_bank):
            banks = []
            for cc in range(2):
                bank = new_bank()
                for j in range(PACK):
                    nc.tensor.transpose(bank[:, j * P : (j + 1) * P], sums_t[:, cc, j * P : (j + 1) * P], ident[:])
                banks.append(bank)
            return banks

        def count_slots(peak):
            present = keep.tile([P, PASSES * PACK * SLOTS], F32, name="present")
            nc.vector.tensor_scalar(out=present[:], in0=peak[:], scalar1=0.0, scalar2=MEAN_SCALE, op0=ALU.is_gt, op1=ALU.mult)
            count = keep.tile([P, PASSES * PACK], F32, name="count")
            nc.vector.tensor_reduce(out=count[:], in_=present[:].rearrange("p (j m) -> p j m", m=SLOTS), axis=AXIS_X, op=ALU.add)
            return count

        def invert(count):
            divisor = keep.tile([P, PASSES * PACK], F32, name="divisor")
            nc.vector.tensor_scalar(out=divisor[:], in0=count[:], scalar1=MEAN_SCALE, scalar2=None, op0=ALU.max)
            inverse = keep.tile([P, PASSES * PACK], F32, name="inverse")
            nc.vector.reciprocal(out=inverse[:], in_=divisor[:])
            return inverse

        def make_mean(g, banks, inverse):
            grouped = grouped_tile()
            for cc in range(2):
                nc.vector.tensor_tensor(
                    out=grouped[:, cc * K_PASS : (cc + 1) * K_PASS].rearrange("p (c j) -> p c j", j=PACK),
                    in0=banks[cc][:].rearrange("p (j c) -> p c j", j=PACK),
                    in1=inverse[:, g * PACK : (g + 1) * PACK].unsqueeze(1).broadcast_to([P, P, PACK]),
                    op=ALU.mult,
                )
            return grouped

        def dw_pass(acc, m, n, g):
            rows = slice(m * P, (m + 1) * P)
            cols = slice(n * BANK, (n + 1) * BANK)
            nc.tensor.matmul_mx(
                out=acc[:],
                lhsT=h_codes[g][:, rows].bitcast(E4M3), lhsT_scale=h_scales[g][:, rows],
                rhs=dz_codes[g][:, cols].bitcast(E5M2), rhs_scale=dz_scales[g][:, cols],
                start=(g == 0), stop=(g == PASSES - 1),
            )

        def open_dw(m, tag, bufs):
            accs = [psum.tile([P, BANK], F32, name="dw_acc", tag=tag, bufs=bufs) for n in range(2)]
            for n in range(2):
                dw_pass(accs[n], m, n, 0)
            return accs

        def close_dw(m, accs, second_copy):
            dw = keep.tile([P, H], F32, name="dw", tag="z%d%d" % (m // 2, m % 2))
            for n in range(2):
                dw_pass(accs[n], m, n, 1)
            nc.scalar.copy(out=dw[:, 0:BANK], in_=accs[0][:])
            second_copy(out=dw[:, BANK:], in_=accs[1][:])
            nc.sync.dma_start(out=out_1[m * P : (m + 1) * P, :], in_=dw[:])

        pairs = [work.tile([P, 2, 2, P, 2], BF16, name="pairs") for g in range(PASSES)]
        sums_t = [work.tile([P, 2, PACK * P], F32, name="sums_t") for g in range(PASSES)]
        peak = keep.tile([P, PASSES * PACK * SLOTS], F32, name="peak")
        tiles = PASSES * PACK
        turned, dzt, woven = {}, {}, {}
        find_peaks([(0, 0)], peak)
        partials = widen_slots(neigh_sb[0, 0], 0)
        w_grouped = [turn_w(hp) for hp in range(2)]
        first_bank = sums_bank()
        add_turned(first_bank, 0, partials)
        partials = widen_slots(neigh_sb[0, 0], 1)
        for i in range(tiles):
            make_slope(i)
            if i < 2:
                quantize_w(i, w_grouped[i])
            elif i >= LAG:
                make_da(i - LAG, quantize_turned(i - LAG, turned[i - LAG]))
            make_dz(i)
            turned[i] = turn_dz(i)
            if i == 0:
                add_turned(first_bank, 1, partials)
                keep_neigh(0, first_bank, sums_t[0])

        make_da(5, quantize_turned(5, turned[5]))
        bank = sum_slots(neigh_sb[0, 1])
        make_da(6, quantize_turned(6, turned[6]))
        keep_neigh(1, bank, sums_t[0])
        make_da(7, quantize_turned(7, turned[7]))
        pair_src(0, sum_slots(src_sb[0, 0]), pairs[0])
        woven[0, 0] = weave_dz(0, 0)
        pair_src(1, sum_slots(src_sb[0, 1]), pairs[0])
        woven[0, 1] = weave_dz(0, 1)
        bank = sum_slots(neigh_sb[1, 0])
        total = [turn_src(pairs[0])]
        keep_neigh(0, bank, sums_t[1])
        sum_src_rows(0, pairs[1])
        bank = sum_slots(neigh_sb[1, 1])
        quantize_dz(0, 0, woven[0, 0])
        woven[1, 0] = weave_dz(1, 0)
        keep_neigh(1, bank, sums_t[1])
        quantize_dz(0, 1, woven[0, 1])
        sum_src_rows(1, pairs[1])
        woven[1, 1] = weave_dz(1, 1)
        banks = [turn_neigh(sums_t[0], sums_bank)]
        total.append(turn_src(pairs[1]))
        banks.append(turn_neigh(sums_t[1], sums_bank))
        quantize_hidden(0, 0, total[0])
        find_peaks([(0, 1), (1, 0), (1, 1)], peak)
        quantize_dz(1, 0, woven[1, 0])
        quantize_dz(1, 1, woven[1, 1])
        count = count_slots(peak)
        quantize_hidden(1, 0, total[1])
        close_dw(0, open_dw(0, "acc", 2), nc.scalar.copy)
        close_dw(1, open_dw(1, "transposed", 2), nc.scalar.copy)
        inverse = invert(count)
        quantize_hidden(0, 1, make_mean(0, banks[0], inverse))
        accs = [open_dw(2, "acc", 2), open_dw(3, "transposed", 2)]
        quantize_hidden(1, 1, make_mean(1, banks[1], inverse))
        for m in range(2, 4):
            close_dw(m, accs[m - 2], nc.vector.tensor_copy)
